import numpy as np
import ml_dtypes


def mxq(x, axis, fmt="e4m3"):
    dtype, down = {"e4m3": (ml_dtypes.float8_e4m3fn, 7), "e5m2": (ml_dtypes.float8_e5m2, 14)}[fmt]
    v = np.moveaxis(np.asarray(x, np.float32).astype(ml_dtypes.bfloat16).astype(np.float64), axis, -1)
    blocks = v.reshape(v.shape[:-1] + (-1, 32))
    amax = np.abs(blocks).max(-1, keepdims=True)
    byte = np.maximum(np.where(amax > 0, np.frexp(amax)[1] - 1 + 127, 0) - down, 1)
    scale = np.exp2(byte - 127.0)
    codes = (blocks / scale).astype(np.float32).astype(dtype).astype(np.float64)
    return np.moveaxis((codes * scale).reshape(v.shape), -1, axis)


WIDE = False


def mx_kscale(k):
    if not WIDE:
        return np.ones(k)
    levels = np.array([10, -10, 5, -5, 0])
    a = np.random.permutation(np.resize(levels, k // 512 * 4)).reshape(k // 512, 4)
    idx = np.arange(k)
    return np.exp2(a[idx // 512, idx % 128 // 32])


BF16 = ml_dtypes.bfloat16


def bf(x):
    return np.asarray(x, np.float32).astype(BF16)


def f64(x):
    return np.asarray(x).astype(np.float64)


B, C, H, W, P, DIM = 8, 8, 128, 128, 16, 768
SHIFT = P // 2
PD = 5 * C * P * P
EPS = 1e-5
XS = 0.015


def patch_shift(x, shift):
    xp = np.pad(x, ((0, 0), (0, 0), (shift, shift), (shift, shift)))
    s2 = 2 * shift
    return np.concatenate([x, xp[:, :, :-s2, :-s2], xp[:, :, :-s2, s2:], xp[:, :, s2:, :-s2], xp[:, :, s2:, s2:]], axis=1)


def patchify(x, p):
    b_, c_, hh, ww = x.shape
    h, w = hh // p, ww // p
    return x.reshape(b_, c_, h, p, w, p).transpose(0, 2, 4, 3, 5, 1).reshape(b_, h * w, p * p * c_)


def layernorm(u, g, b):
    m = u.mean(-1, keepdims=True)
    v = np.square(u - m).mean(-1, keepdims=True)
    return (u - m) / np.sqrt(v + EPS) * g + b


def setup_inputs():
    s = mx_kscale(PD)
    return {"x": bf(np.random.standard_normal((B, C, H, W)) * XS),
            "ln1_g": bf((1.0 + 0.1 * np.random.standard_normal(PD)) * s),
            "ln1_b": bf(0.1 * np.random.standard_normal(PD) * s),
            "w1": bf(np.random.standard_normal((PD, DIM)) / np.sqrt(PD) / s[:, None]),
            "b1": bf(0.3 * np.random.standard_normal(DIM))}


def reference(x, ln1_g, ln1_b, w1, b1):
    u = patchify(patch_shift(f64(x), SHIFT), P)
    z = layernorm(u, f64(ln1_g), f64(ln1_b))
    return (mxq(z, 2, "e4m3") @ mxq(f64(w1), 0, "e4m3")) + f64(b1)

@@ -1,0 +1,267 @@
+from contextlib import ExitStack
+
+import concourse.bass as bass
+import concourse.mybir as mybir
+import concourse.tile as tile
+from concourse.masks import make_identity
+
+F32 = mybir.dt.float32
+BF16 = mybir.dt.bfloat16
+U32 = mybir.dt.uint32
+U8 = mybir.dt.uint8
+FP8X4 = mybir.dt.float8_e4m3fn_x4
+ALU = mybir.AluOpType
+ACT = mybir.ActivationFunctionType
+AX = mybir.AxisListType
+
+P = 128
+B, C, HW, PATCH, DIM = 8, 8, 128, 16, 768
+PD = 5 * C * PATCH * PATCH
+EPS = 1e-5
+FLOPS = 2 * B * 64 * PD * DIM
+SHIFTS = ((0, 0), (-1, -1), (-1, 1), (1, -1), (1, 1))
+RUNS = 40
+CHUNK_RUNS = 10
+S1_SCALAR = ((0, 1, 2, 3, 4), (4,))
+W_VEC_COLS = 672
+
+
+def tile_shiftedpatchtokenization_pa_kernel(tc, x, ln1_g, ln1_b, w1, b1, out):
+    nc = tc.nc
+    with ExitStack() as ctx:
+        consts = ctx.enter_context(tc.tile_pool(name="consts", bufs=1))
+        wraw_pool = ctx.enter_context(tc.tile_pool(name="wraw", bufs=3))
+        wi_pool = ctx.enter_context(tc.tile_pool(name="wi", bufs=2))
+        xh_pool = ctx.enter_context(tc.tile_pool(name="xh", bufs=8))
+        zp_pool = ctx.enter_context(tc.tile_pool(name="zp", bufs=2))
+        zi_pool = ctx.enter_context(tc.tile_pool(name="zi", bufs=2))
+        zc_pool = ctx.enter_context(tc.tile_pool(name="zc", bufs=3))
+        junk_pool = ctx.enter_context(tc.tile_pool(name="junk", bufs=1))
+        acc_pool = ctx.enter_context(tc.psum_pool(name="acc", bufs=1))
+        tp_pool = ctx.enter_context(tc.psum_pool(name="tp", bufs=4))
+
+        w_codes = [consts.tile([P, DIM], U32, name="wc%d" % g, align_bytes=64) for g in range(20)]
+        w_scales = [consts.tile([P, DIM], U8, name="ws%d" % g, align_bytes=64) for g in range(20)]
+        w_raw = {}
+
+        def load_w(g):
+            wr = wraw_pool.tile([P, 4, DIM], BF16, name="wr")
+            nc.sync.dma_start(out=wr[:], in_=w1[512 * g:512 * g + 512, :].rearrange("(t p) n -> p t n", p=P))
+            w_raw[g] = wr
+
+        def load_nth_w(n):
+            load_w(10 * (n % 2) + n // 2)
+
+        load_nth_w(0)
+        load_nth_w(1)
+        xc = consts.tile([P, C, 8, HW], BF16, name="xc")
+        xu = consts.tile([P, C, 8, HW], BF16, name="xu")
+        xd = consts.tile([P, C, 8, HW], BF16, name="xd")
+        for b in range(B):
+            queue = nc.sync if b < 4 else nc.scalar
+            queue.dma_start(
+                out=xc[b:P:8, :, :, :].rearrange("p c q w -> p c (q w)"), in_=x[b].rearrange("c (r q) w -> r c (q w)", q=8)
+            )
+        load_nth_w(2)
+        graw = consts.tile([P, P], BF16, name="graw")
+        braw = consts.tile([P, P], BF16, name="braw")
+        nc.vector.memset(graw[:], 0.0)
+        nc.vector.memset(braw[:], 0.0)
+        nc.scalar.dma_start(out=graw[0:80, :], in_=ln1_g.rearrange("(r p) -> r p", p=P))
+        nc.scalar.dma_start(out=braw[0:80, :], in_=ln1_b.rearrange("(r p) -> r p", p=P))
+        b1b = consts.tile([P, DIM], BF16, name="b1b")
+        nc.scalar.dma_start(out=b1b[:], in_=b1.partition_broadcast(P))
+
+        eye = consts.tile([P, P], F32, name="eye")
+        make_identity(nc, eye[:])
+        eye4 = eye[:].rearrange("p (i a b) -> p i a b", a=2, b=8)
+        perm = consts.tile([P, P], F32, name="perm")
+        nc.vector.tensor_copy(
+            out=perm[:].rearrange("p (a b i) -> p a b i", a=2, b=8),
+            in_=eye[:].rearrange("p (i a b) -> p a b i", a=2, b=8),
+        )
+        rot_up = consts.tile([P, P], BF16, name="rot_up")
+        rot_dn = consts.tile([P, P], BF16, name="rot_dn")
+        nc.vector.memset(rot_up[:], 0.0)
+        nc.vector.memset(rot_dn[:], 0.0)
+        nc.vector.tensor_copy(out=rot_up[:, 8:P], in_=eye[:, 0:120])
+        nc.vector.tensor_copy(out=rot_dn[:, 0:120], in_=eye[:, 8:P])
+        tok2 = consts.tile([P, 8, 8], F32, name="tok2")
+        tok4 = consts.tile([P, 8, 8], F32, name="tok4")
+        nc.vector.tensor_add(out=tok2[:], in0=eye4[:, :, 0, :], in1=eye4[:, :, 1, :])
+        nc.vector.tensor_copy(out=tok4[:], in_=tok2[:])
+        nc.vector.tensor_add(out=tok4[:, 1:8, :], in0=tok4[:, 1:8, :], in1=eye4[:, 0:7, 1, :])
+        nc.vector.tensor_add(out=tok4[:, 0:7, :], in0=tok4[:, 0:7, :], in1=eye4[:, 1:8, 0, :])
+        rows4 = consts.tile([P, P], F32, name="rows4")
+        rows2 = consts.tile([P, P], F32, name="rows2")
+        for a in range(2):
+            nc.vector.tensor_copy(out=rows4[:].rearrange("p (i a b) -> p i a b", a=2, b=8)[:, :, a, :], in_=tok4[:])
+            nc.vector.tensor_copy(out=rows2[:].rearrange("p (i a b) -> p i a b", a=2, b=8)[:, :, a, :], in_=tok2[:])
+
+        gk = consts.tile([P, 80], F32, name="gk")
+        bk = consts.tile([P, 80], F32, name="bk")
+        for raw, dst, nm in ((graw, gk, "gf"), (braw, bk, "bf")):
+            wide = consts.tile([P, P], F32, name=nm)
+            nc.vector.tensor_copy(out=wide[:], in_=raw[:])
+            pt = tp_pool.tile([P, 4, P], F32, name="tp")
+            nc.tensor.transpose(out=pt[:, 0, :], in_=wide[:], identity=eye[:])
+            nc.vector.tensor_copy(out=dst[:], in_=pt[:, 0, 0:80])
+
+        part1 = consts.tile([P, C, 16], F32, name="part1")
+        sq = consts.tile([P, 16], F32, name="sq")
+        cells = consts.tile([P, 2, 16], F32, name="cells")
+        for c in range(C):
+            nc.vector.tensor_reduce(
+                out=part1[:, c, :],
+                in_=xc[:, c, :, :].rearrange("p q (j r) -> p j q r", r=8),
+                axis=AX.XY,
+                op=ALU.add,
+            )
+        for j in range(16):
+            junk = junk_pool.tile([P, C, 8, 8], BF16, name="junk")
+            nc.scalar.activation(
+                out=junk[:], in_=xc[:, :, :, 8 * j:8 * j + 8], func=ACT.Square, accum_out=sq[:, j:j + 1]
+            )
+        xc_flat = xc[:].rearrange("p c q w -> p (c q w)")
+        n_copy = 0
+        for m in range(C):
+            for rot, dst in ((rot_up, xu), (rot_dn, xd)):
+                ps = tp_pool.tile([P, 1024], BF16, name="tp")
+                for h in range(2):
+                    lo = 1024 * m + 512 * h
+                    nc.tensor.matmul(out=ps[:, 512 * h:512 * h + 512], lhsT=rot[:], rhs=xc_flat[:, lo:lo + 512], start=True, stop=True)
+                dflat = dst[:].rearrange("p c q w -> p (c q w)")[:, 1024 * m:1024 * m + 1024]
+                if n_copy % 2 == 0:
+                    nc.scalar.copy(out=dflat, in_=ps[:])
+                else:
+                    nc.vector.tensor_copy(out=dflat, in_=ps[:])
+                n_copy += 1
+        nc.vector.tensor_reduce(out=cells[:, 0, :], in_=part1[:].rearrange("p c j -> p j c"), axis=AX.X, op=ALU.add)
+        nc.vector.tensor_copy(out=cells[:, 1, :], in_=sq[:])
+        st = tp_pool.tile([P, 4, P], F32, name="tp")
+        nc.tensor.matmul(out=st[:, 0, 0:32], lhsT=rows4[:], rhs=cells[:].rearrange("p s j -> p (s j)"), start=True, stop=True)
+        nc.tensor.matmul(out=st[:, 0, 32:64], lhsT=rows2[:], rhs=cells[:].rearrange("p s j -> p (s j)"), start=True, stop=True)
+        padded = consts.tile([P, 4, 18], F32, name="padded")
+        nc.vector.memset(padded[:], 0.0)
+        nc.vector.tensor_copy(out=padded[:, :, 1:17], in_=st[:, 0, 0:64].rearrange("p (k j) -> p k j", j=16))
+        pairs = consts.tile([P, 2, 9], F32, name="pairs")
+        inner = consts.tile([P, 2, 8], F32, name="inner")
+        tot = consts.tile([P, 2, 8], F32, name="tot")
+        nc.vector.tensor_add(out=pairs[:], in0=padded[:, 0:2, 0:18:2], in1=padded[:, 0:2, 1:18:2])
+        nc.vector.tensor_add(out=inner[:], in0=padded[:, 2:4, 1:17:2], in1=padded[:, 2:4, 2:18:2])
+        nc.vector.tensor_add(out=tot[:], in0=pairs[:, :, 0:8], in1=pairs[:, :, 1:9])
+        nc.vector.tensor_add(out=tot[:], in0=tot[:], in1=inner[:])
+        mean = consts.tile([P, 8], F32, name="mean")
+        msq = consts.tile([P, 8], F32, name="msq")
+        var = consts.tile([P, 8], F32, name="var")
+        std = consts.tile([P, 8], F32, name="std")
+        r0 = consts.tile([P, 8], F32, name="r0")
+        nt = consts.tile([P, 8], F32, name="nt")
+        rstd = consts.tile([P, 8], F32, name="rstd")
+        nmr = consts.tile([P, 8], F32, name="nmr")
+        nc.vector.tensor_scalar_mul(out=mean[:], in0=tot[:, 0, :], scalar1=1.0 / PD)
+        nc.vector.tensor_mul(out=msq[:], in0=mean[:], in1=mean[:])
+        nc.vector.scalar_tensor_tensor(out=var[:], in0=tot[:, 1, :], scalar=1.0 / PD, in1=msq[:], op0=ALU.mult, op1=ALU.subtract)
+        nc.vector.tensor_scalar(out=var[:], in0=var[:], scalar1=0.0, scalar2=EPS, op0=ALU.max, op1=ALU.add)
+        nc.scalar.sqrt(out=std[:], in_=var[:])
+        nc.vector.reciprocal(out=r0[:], in_=std[:])
+        nc.vector.tensor_mul(out=nt[:], in0=r0[:], in1=r0[:])
+        nc.vector.tensor_mul(out=nt[:], in0=nt[:], in1=var[:])
+        nc.vector.tensor_scalar(out=nt[:], in0=nt[:], scalar1=-0.5, scalar2=1.5, op0=ALU.mult, op1=ALU.add)
+        nc.vector.tensor_mul(out=rstd[:], in0=r0[:], in1=nt[:])
+        nc.vector.scalar_tensor_tensor(out=nmr[:], in0=mean[:], scalar=-1.0, in1=rstd[:], op0=ALU.mult, op1=ALU.mult)
+
+        def regroup4(copy, dst, src):
+            copy(out=dst.rearrange("p (c i) t -> p c t i", i=4), in_=src.rearrange("p t (c i) -> p c t i", i=4))
+
+        def produce_w(g):
+            wr = w_raw.pop(g)
+            wi = wi_pool.tile([P, DIM, 4], BF16, name="wi", align_bytes=64)
+            regroup4(nc.vector.tensor_copy, wi[:, 0:W_VEC_COLS, :], wr[:, :, 0:W_VEC_COLS])
+            regroup4(nc.scalar.copy, wi[:, W_VEC_COLS:DIM, :], wr[:, :, W_VEC_COLS:DIM])
+            flat = wi[:].rearrange("p n t -> p (n t)")
+            for lo, hi in ((0, 512), (512, 768)):
+                nc.vector.quantize_mx(
+                    out=w_codes[g][:, lo:hi].bitcast(FP8X4), scales=w_scales[g][:, lo:hi], in_=flat[:, 4 * lo:4 * hi]
+                )
+
+        def affine(engine_is_scalar, dst, src, scale, bias):
+            if engine_is_scalar:
+                nc.scalar.activation(out=dst, in_=src, func=ACT.Identity, bias=bias, scale=scale)
+            else:
+                nc.vector.tensor_scalar(out=dst, in0=src, scalar1=scale, scalar2=bias, op0=ALU.mult, op1=ALU.add)
+
+        def stage1(half, chunk):
+            tiles = []
+            for jj in range(4):
+                j = 4 * half + jj
+                xh = xh_pool.tile([P, 1280], F32, name="xh")
+                view = xh[:].rearrange("p (q e s c) -> p q e s c", q=2, e=16, s=5)
+                for s, (di, dj) in enumerate(SHIFTS):
+                    row0 = 2 * chunk
+                    x3 = (xu, xc, xd)[di + 1]
+                    col0 = 16 * j + 8 * dj
+                    lo = 8 if col0 < 0 else 0
+                    hi = 8 if col0 + 16 > HW else 16
+                    on_scalar = s in S1_SCALAR[half]
+                    for ch in range(2):
+                        src = x3[:, 4 * ch:4 * ch + 4, row0:row0 + 2, col0 + lo:col0 + hi].rearrange("p c q e -> p q e c")
+                        affine(on_scalar, view[:, :, lo:hi, s, 4 * ch:4 * ch + 4], src, rstd[:, j:j + 1], nmr[:, j:j + 1])
+                        if hi - lo < 16:
+                            plo, phi = (0, 8) if lo == 8 else (8, 16)
+                            affine(on_scalar, view[:, :, plo:phi, s, 4 * ch:4 * ch + 4], src, 0.0, nmr[:, j:j + 1])
+                tiles.append(xh)
+            return tiles
+
+        out_rows = out.rearrange("b (i j) n -> j (b i) n", j=8)
+        for half in range(2):
+            acc = [acc_pool.tile([P, 512], F32, name="acc%d" % k) for k in range(4)]
+            tiles = None
+            for mu in range(10):
+                if half == 0:
+                    for a in range(2):
+                        produce_w(10 * a + mu)
+                        if 2 * mu + a + 3 < 20:
+                            load_nth_w(2 * mu + a + 3)
+                zp = zp_pool.tile([P, 2, 4, 256], BF16, name="zp")
+                for t in range(4):
+                    r = 4 * mu + t
+                    if r % CHUNK_RUNS == 0:
+                        tiles = stage1(half, r // CHUNK_RUNS)
+                    pt = tp_pool.tile([P, 4, P], F32, name="tp")
+                    off = P * (r % CHUNK_RUNS)
+                    for jj in range(4):
+                        nc.tensor.transpose(out=pt[:, jj, :], in_=tiles[jj][:, off:off + P], identity=perm[:])
+                    for a in range(2):
+                        k = 40 * a + r
+                        affine(True, zp[:, a, t, :].rearrange("p (j m) -> p j m", j=4), pt[:, :, 64 * a:64 * a + 64],
+                               gk[:, k:k + 1], bk[:, k:k + 1])
+                zi = zi_pool.tile([P, 2, 256, 4], BF16, name="zi", align_bytes=64)
+                nc.vector.tensor_copy(
+                    out=zi[:].rearrange("p a (c i) t -> p a c t i", i=4), in_=zp[:].rearrange("p a t (c i) -> p a c t i", i=4)
+                )
+                zc = zc_pool.tile([P, 512], U32, name="zc", align_bytes=64)
+                zs = zc_pool.tile([P, 512], U8, name="zs", align_bytes=64)
+                nc.vector.quantize_mx(out=zc[:].bitcast(FP8X4), scales=zs[:], in_=zi[:].rearrange("p a m t -> p (a m t)"))
+                for a in range(2):
+                    g = 10 * a + mu
+                    first = mu == 0 and a == 0
+                    last = mu == 9 and a == 1
+                    for tt in range(2):
+                        cols = slice(256 * a + P * tt, 256 * a + P * tt + P)
+                        for dst, lo, hi in ((acc[2 * tt], 0, 512), (acc[2 * tt + 1], 512, 768)):
+                            nc.tensor.matmul_mx(
+                                out=dst[:, 0:hi - lo],
+                                lhsT=zc[:, cols].bitcast(FP8X4),
+                                lhsT_scale=zs[:, cols],
+                                rhs=w_codes[g][:, lo:hi].bitcast(FP8X4),
+                                rhs_scale=w_scales[g][:, lo:hi],
+                                start=first,
+                                stop=last,
+                            )
+            for tt in range(2):
+                o = xh_pool.tile([P, DIM], F32, name="xh")
+                nc.vector.tensor_tensor(out=o[:, 0:512], in0=acc[2 * tt][:], in1=b1b[:, 0:512], op=ALU.add)
+                nc.vector.tensor_tensor(out=o[:, 512:768], in0=acc[2 * tt + 1][:, 0:256], in1=b1b[:, 512:768], op=ALU.add)
+                for jl in range(2):
+                    nc.sync.dma_start(out=out_rows[4 * half + 2 * tt + jl], in_=o[64 * jl:64 * jl + 64, :])

@@ -1,8 +1,6 @@
 from contextlib import ExitStack
 
-import concourse.bass as bass
 import concourse.mybir as mybir
-import concourse.tile as tile
 from concourse.masks import make_identity
 
 F32 = mybir.dt.float32
@@ -12,23 +10,25 @@ U8 = mybir.dt.uint8
 FP8X4 = mybir.dt.float8_e4m3fn_x4
 ALU = mybir.AluOpType
 ACT = mybir.ActivationFunctionType
-AX = mybir.AxisListType
 
 P = 128
-B, C, HW, PATCH, DIM = 8, 8, 128, 16, 768
-PD = 5 * C * PATCH * PATCH
+B, C, HW, DIM = 8, 8, 128, 768
+PD = 10240
 EPS = 1e-5
 FLOPS = 2 * B * 64 * PD * DIM
 SHIFTS = ((0, 0), (-1, -1), (-1, 1), (1, -1), (1, 1))
-RUNS = 40
-CHUNK_RUNS = 10
-S1_SCALAR = ((0, 1, 2, 3, 4), (4,))
-W_VEC_COLS = 672
+PASSES = 20
+UNITS = 20
+HEAD_PASSES = 5
+LEAD_TILES = 5
+HEAD_SCALAR_COLS = 256
+BODY_SCALAR_COLS = 96
 
 
 def tile_shiftedpatchtokenization_pa_kernel(tc, x, ln1_g, ln1_b, w1, b1, out):
     nc = tc.nc
     with ExitStack() as ctx:
+        ctx.enter_context(tc.manual_schedule())
         consts = ctx.enter_context(tc.tile_pool(name="consts", bufs=1))
         wraw_pool = ctx.enter_context(tc.tile_pool(name="wraw", bufs=3))
         wi_pool = ctx.enter_context(tc.tile_pool(name="wi", bufs=2))
@@ -36,33 +36,54 @@ def tile_shiftedpatchtokenization_pa_kernel(tc, x, ln1_g, ln1_b, w1, b1, out):
         zp_pool = ctx.enter_context(tc.tile_pool(name="zp", bufs=2))
         zi_pool = ctx.enter_context(tc.tile_pool(name="zi", bufs=2))
         zc_pool = ctx.enter_context(tc.tile_pool(name="zc", bufs=3))
-        junk_pool = ctx.enter_context(tc.tile_pool(name="junk", bufs=1))
+        o_pool = ctx.enter_context(tc.tile_pool(name="o", bufs=2))
         acc_pool = ctx.enter_context(tc.psum_pool(name="acc", bufs=1))
         tp_pool = ctx.enter_context(tc.psum_pool(name="tp", bufs=4))
 
-        w_codes = [consts.tile([P, DIM], U32, name="wc%d" % g, align_bytes=64) for g in range(20)]
-        w_scales = [consts.tile([P, DIM], U8, name="ws%d" % g, align_bytes=64) for g in range(20)]
+        w_codes = [consts.tile([P, DIM], U32, name="wc%d" % g, align_bytes=64) for g in range(PASSES)]
+        w_scales = [consts.tile([P, DIM], U8, name="ws%d" % g, align_bytes=64) for g in range(PASSES)]
         w_raw = {}
+        w_grouped = {}
 
-        def load_w(g):
-            wr = wraw_pool.tile([P, 4, DIM], BF16, name="wr")
-            nc.sync.dma_start(out=wr[:], in_=w1[512 * g:512 * g + 512, :].rearrange("(t p) n -> p t n", p=P))
-            w_raw[g] = wr
+        def nth_pass(n):
+            return 10 * (n % 2) + n // 2
 
-        def load_nth_w(n):
-            load_w(10 * (n % 2) + n // 2)
+        def load_w(n):
+            if n < PASSES:
+                g = nth_pass(n)
+                wr = wraw_pool.tile([P, 4, DIM], BF16, name="wr")
+                nc.sync.dma_start(out=wr[:], in_=w1[512 * g:512 * g + 512, :].rearrange("(t p) n -> p t n", p=P))
+                w_raw[n] = wr
 
-        load_nth_w(0)
-        load_nth_w(1)
+        def regroup4(copy, dst, src):
+            copy(out=dst.rearrange("p (c i) t -> p c t i", i=4), in_=src.rearrange("p t (c i) -> p c t i", i=4))
+
+        def regroup_w(n, scalar_cols):
+            wr = w_raw.pop(n)
+            wi = wi_pool.tile([P, DIM, 4], BF16, name="wi", align_bytes=64)
+            cut = DIM - scalar_cols
+            regroup4(nc.scalar.copy, wi[:, cut:DIM, :], wr[:, :, cut:DIM])
+            regroup4(nc.vector.tensor_copy, wi[:, 0:cut, :], wr[:, :, 0:cut])
+            w_grouped[n] = wi
+            load_w(n + 3)
+
+        def quantise_w(n):
+            g = nth_pass(n)
+            flat = w_grouped.pop(n)[:].rearrange("p n t -> p (n t)")
+            for lo, hi in ((0, 512), (512, 768)):
+                nc.vector.quantize_mx(
+                    out=w_codes[g][:, lo:hi].bitcast(FP8X4), scales=w_scales[g][:, lo:hi], in_=flat[:, 4 * lo:4 * hi]
+                )
+
+        for n in range(3):
+            load_w(n)
         xc = consts.tile([P, C, 8, HW], BF16, name="xc")
         xu = consts.tile([P, C, 8, HW], BF16, name="xu")
         xd = consts.tile([P, C, 8, HW], BF16, name="xd")
         for b in range(B):
-            queue = nc.sync if b < 4 else nc.scalar
-            queue.dma_start(
+            nc.scalar.dma_start(
                 out=xc[b:P:8, :, :, :].rearrange("p c q w -> p c (q w)"), in_=x[b].rearrange("c (r q) w -> r c (q w)", q=8)
             )
-        load_nth_w(2)
         graw = consts.tile([P, P], BF16, name="graw")
         braw = consts.tile([P, P], BF16, name="braw")
         nc.vector.memset(graw[:], 0.0)
@@ -77,8 +98,7 @@ def tile_shiftedpatchtokenization_pa_kernel(tc, x, ln1_g, ln1_b, w1, b1, out):
         eye4 = eye[:].rearrange("p (i a b) -> p i a b", a=2, b=8)
         perm = consts.tile([P, P], F32, name="perm")
         nc.vector.tensor_copy(
-            out=perm[:].rearrange("p (a b i) -> p a b i", a=2, b=8),
-            in_=eye[:].rearrange("p (i a b) -> p a b i", a=2, b=8),
+            out=perm[:].rearrange("p (a b i) -> p a b i", a=2, b=8), in_=eye[:].rearrange("p (i a b) -> p a b i", a=2, b=8)
         )
         rot_up = consts.tile([P, P], BF16, name="rot_up")
         rot_dn = consts.tile([P, P], BF16, name="rot_dn")
@@ -97,6 +117,13 @@ def tile_shiftedpatchtokenization_pa_kernel(tc, x, ln1_g, ln1_b, w1, b1, out):
         for a in range(2):
             nc.vector.tensor_copy(out=rows4[:].rearrange("p (i a b) -> p i a b", a=2, b=8)[:, :, a, :], in_=tok4[:])
             nc.vector.tensor_copy(out=rows2[:].rearrange("p (i a b) -> p i a b", a=2, b=8)[:, :, a, :], in_=tok2[:])
+        padded = consts.tile([P, 4, 18], F32, name="padded")
+        nc.vector.memset(padded[:], 0.0)
+
+        regroup_w(0, HEAD_SCALAR_COLS)
+        for n in range(1, HEAD_PASSES):
+            regroup_w(n, HEAD_SCALAR_COLS)
+            quantise_w(n - 1)
 
         gk = consts.tile([P, 80], F32, name="gk")
         bk = consts.tile([P, 80], F32, name="bk")
@@ -106,43 +133,32 @@ def tile_shiftedpatchtokenization_pa_kernel(tc, x, ln1_g, ln1_b, w1, b1, out):
             pt = tp_pool.tile([P, 4, P], F32, name="tp")
             nc.tensor.transpose(out=pt[:, 0, :], in_=wide[:], identity=eye[:])
             nc.vector.tensor_copy(out=dst[:], in_=pt[:, 0, 0:80])
+        quantise_w(HEAD_PASSES - 1)
 
-        part1 = consts.tile([P, C, 16], F32, name="part1")
-        sq = consts.tile([P, 16], F32, name="sq")
-        cells = consts.tile([P, 2, 16], F32, name="cells")
-        for c in range(C):
-            nc.vector.tensor_reduce(
-                out=part1[:, c, :],
-                in_=xc[:, c, :, :].rearrange("p q (j r) -> p j q r", r=8),
-                axis=AX.XY,
-                op=ALU.add,
-            )
+        st6 = consts.tile([P, 16, 6], F32, name="st6")
         for j in range(16):
-            junk = junk_pool.tile([P, C, 8, 8], BF16, name="junk")
-            nc.scalar.activation(
-                out=junk[:], in_=xc[:, :, :, 8 * j:8 * j + 8], func=ACT.Square, accum_out=sq[:, j:j + 1]
-            )
+            nc.vector.bn_stats(out=st6[:, j, :], in_=xc[:, :, :, 8 * j:8 * j + 8])
         xc_flat = xc[:].rearrange("p c q w -> p (c q w)")
-        n_copy = 0
         for m in range(C):
             for rot, dst in ((rot_up, xu), (rot_dn, xd)):
                 ps = tp_pool.tile([P, 1024], BF16, name="tp")
                 for h in range(2):
                     lo = 1024 * m + 512 * h
                     nc.tensor.matmul(out=ps[:, 512 * h:512 * h + 512], lhsT=rot[:], rhs=xc_flat[:, lo:lo + 512], start=True, stop=True)
-                dflat = dst[:].rearrange("p c q w -> p (c q w)")[:, 1024 * m:1024 * m + 1024]
-                if n_copy % 2 == 0:
-                    nc.scalar.copy(out=dflat, in_=ps[:])
-                else:
-                    nc.vector.tensor_copy(out=dflat, in_=ps[:])
-                n_copy += 1
-        nc.vector.tensor_reduce(out=cells[:, 0, :], in_=part1[:].rearrange("p c j -> p j c"), axis=AX.X, op=ALU.add)
-        nc.vector.tensor_copy(out=cells[:, 1, :], in_=sq[:])
+                nc.scalar.copy(out=dst[:].rearrange("p c q w -> p (c q w)")[:, 1024 * m:1024 * m + 1024], in_=ps[:])
+        halves = st6[:].rearrange("p j (h k) -> p j h k", h=2)
+        cells = consts.tile([P, 2, 16], F32, name="cells")
+        sqm = consts.tile([P, 16, 2], F32, name="sqm")
+        s2 = consts.tile([P, 16], F32, name="s2")
+        m2 = consts.tile([P, 16], F32, name="m2")
+        nc.vector.tensor_add(out=cells[:, 0, :], in0=halves[:, :, 0, 1], in1=halves[:, :, 1, 1])
+        nc.vector.tensor_mul(out=sqm[:], in0=halves[:, :, :, 1], in1=halves[:, :, :, 1])
+        nc.vector.tensor_add(out=m2[:], in0=halves[:, :, 0, 2], in1=halves[:, :, 1, 2])
+        nc.vector.tensor_add(out=s2[:], in0=sqm[:, :, 0], in1=sqm[:, :, 1])
+        nc.vector.scalar_tensor_tensor(out=cells[:, 1, :], in0=s2[:], scalar=256.0, in1=m2[:], op0=ALU.mult, op1=ALU.add)
         st = tp_pool.tile([P, 4, P], F32, name="tp")
         nc.tensor.matmul(out=st[:, 0, 0:32], lhsT=rows4[:], rhs=cells[:].rearrange("p s j -> p (s j)"), start=True, stop=True)
         nc.tensor.matmul(out=st[:, 0, 32:64], lhsT=rows2[:], rhs=cells[:].rearrange("p s j -> p (s j)"), start=True, stop=True)
-        padded = consts.tile([P, 4, 18], F32, name="padded")
-        nc.vector.memset(padded[:], 0.0)
         nc.vector.tensor_copy(out=padded[:, :, 1:17], in_=st[:, 0, 0:64].rearrange("p (k j) -> p k j", j=16))
         pairs = consts.tile([P, 2, 9], F32, name="pairs")
         inner = consts.tile([P, 2, 8], F32, name="inner")
@@ -151,15 +167,11 @@ def tile_shiftedpatchtokenization_pa_kernel(tc, x, ln1_g, ln1_b, w1, b1, out):
         nc.vector.tensor_add(out=inner[:], in0=padded[:, 2:4, 1:17:2], in1=padded[:, 2:4, 2:18:2])
         nc.vector.tensor_add(out=tot[:], in0=pairs[:, :, 0:8], in1=pairs[:, :, 1:9])
         nc.vector.tensor_add(out=tot[:], in0=tot[:], in1=inner[:])
-        mean = consts.tile([P, 8], F32, name="mean")
-        msq = consts.tile([P, 8], F32, name="msq")
-        var = consts.tile([P, 8], F32, name="var")
-        std = consts.tile([P, 8], F32, name="std")
-        r0 = consts.tile([P, 8], F32, name="r0")
-        nt = consts.tile([P, 8], F32, name="nt")
-        rstd = consts.tile([P, 8], F32, name="rstd")
-        nmr = consts.tile([P, 8], F32, name="nmr")
-        nc.vector.tensor_scalar_mul(out=mean[:], in0=tot[:, 0, :], scalar1=1.0 / PD)
+        small = {}
+        for nm in ("mean", "msq", "var", "std", "r0", "nt", "rstd", "nmr"):
+            small[nm] = consts.tile([P, 8], F32, name=nm)
+        mean, msq, var, std, r0, nt, rstd, nmr = (small[nm] for nm in ("mean", "msq", "var", "std", "r0", "nt", "rstd", "nmr"))
+        nc.vector.tensor_scalar_mul(out=mean[:], in0=tot[:, 0, :], scalar1=256.0 / PD)
         nc.vector.tensor_mul(out=msq[:], in0=mean[:], in1=mean[:])
         nc.vector.scalar_tensor_tensor(out=var[:], in0=tot[:, 1, :], scalar=1.0 / PD, in1=msq[:], op0=ALU.mult, op1=ALU.subtract)
         nc.vector.tensor_scalar(out=var[:], in0=var[:], scalar1=0.0, scalar2=EPS, op0=ALU.max, op1=ALU.add)
@@ -171,97 +183,128 @@ def tile_shiftedpatchtokenization_pa_kernel(tc, x, ln1_g, ln1_b, w1, b1, out):
         nc.vector.tensor_mul(out=rstd[:], in0=r0[:], in1=nt[:])
         nc.vector.scalar_tensor_tensor(out=nmr[:], in0=mean[:], scalar=-1.0, in1=rstd[:], op0=ALU.mult, op1=ALU.mult)
 
-        def regroup4(copy, dst, src):
-            copy(out=dst.rearrange("p (c i) t -> p c t i", i=4), in_=src.rearrange("p t (c i) -> p c t i", i=4))
-
-        def produce_w(g):
-            wr = w_raw.pop(g)
-            wi = wi_pool.tile([P, DIM, 4], BF16, name="wi", align_bytes=64)
-            regroup4(nc.vector.tensor_copy, wi[:, 0:W_VEC_COLS, :], wr[:, :, 0:W_VEC_COLS])
-            regroup4(nc.scalar.copy, wi[:, W_VEC_COLS:DIM, :], wr[:, :, W_VEC_COLS:DIM])
-            flat = wi[:].rearrange("p n t -> p (n t)")
-            for lo, hi in ((0, 512), (512, 768)):
-                nc.vector.quantize_mx(
-                    out=w_codes[g][:, lo:hi].bitcast(FP8X4), scales=w_scales[g][:, lo:hi], in_=flat[:, 4 * lo:4 * hi]
-                )
-
-        def affine(engine_is_scalar, dst, src, scale, bias):
-            if engine_is_scalar:
+        def affine(on_scalar, dst, src, scale, bias):
+            if on_scalar:
                 nc.scalar.activation(out=dst, in_=src, func=ACT.Identity, bias=bias, scale=scale)
             else:
                 nc.vector.tensor_scalar(out=dst, in0=src, scalar1=scale, scalar2=bias, op0=ALU.mult, op1=ALU.add)
 
-        def stage1(half, chunk):
-            tiles = []
-            for jj in range(4):
-                j = 4 * half + jj
-                xh = xh_pool.tile([P, 1280], F32, name="xh")
-                view = xh[:].rearrange("p (q e s c) -> p q e s c", q=2, e=16, s=5)
-                for s, (di, dj) in enumerate(SHIFTS):
-                    row0 = 2 * chunk
-                    x3 = (xu, xc, xd)[di + 1]
-                    col0 = 16 * j + 8 * dj
-                    lo = 8 if col0 < 0 else 0
-                    hi = 8 if col0 + 16 > HW else 16
-                    on_scalar = s in S1_SCALAR[half]
-                    for ch in range(2):
-                        src = x3[:, 4 * ch:4 * ch + 4, row0:row0 + 2, col0 + lo:col0 + hi].rearrange("p c q e -> p q e c")
-                        affine(on_scalar, view[:, :, lo:hi, s, 4 * ch:4 * ch + 4], src, rstd[:, j:j + 1], nmr[:, j:j + 1])
-                        if hi - lo < 16:
-                            plo, phi = (0, 8) if lo == 8 else (8, 16)
-                            affine(on_scalar, view[:, :, plo:phi, s, 4 * ch:4 * ch + 4], src, 0.0, nmr[:, j:j + 1])
-                tiles.append(xh)
-            return tiles
+        xh_tiles = {}
+
+        def normalise(k, n_scalar):
+            j = 4 * (k // 16) + k % 4
+            chunk = (k % 16) // 4
+            xh = xh_pool.tile([P, 1280], F32, name="xh")
+            view = xh[:].rearrange("p (q e s c) -> p q e s c", q=2, e=16, s=5)
+            for s, (di, dj) in enumerate(SHIFTS):
+                source = (xu, xc, xd)[di + 1]
+                col0 = 16 * j + 8 * dj
+                lo = 8 if col0 < 0 else 0
+                hi = 8 if col0 + 16 > HW else 16
+                on_scalar = s >= 5 - n_scalar
+                for ch in range(2):
+                    src = source[:, 4 * ch:4 * ch + 4, 2 * chunk:2 * chunk + 2, col0 + lo:col0 + hi].rearrange("p c q e -> p q e c")
+                    affine(on_scalar, view[:, :, lo:hi, s, 4 * ch:4 * ch + 4], src, rstd[:, j:j + 1], nmr[:, j:j + 1])
+                    if hi - lo < 16:
+                        affine(on_scalar, view[:, :, 8 - lo:24 - hi, s, 4 * ch:4 * ch + 4], src, 0.0, nmr[:, j:j + 1])
+            xh_tiles[k] = xh
+
+        banks, planes, grouped, z_codes, acc = {}, {}, {}, {}, {}
+
+        def transposes(u):
+            banks[u] = []
+            for t in range(4):
+                run = 4 * u + t
+                pt = tp_pool.tile([P, 4, P], F32, name="tp")
+                for jj in range(4):
+                    nc.tensor.transpose(
+                        out=pt[:, jj, :], in_=xh_tiles[4 * (run // 10) + jj][:, P * (run % 10):P * (run % 10) + P], identity=perm[:]
+                    )
+                banks[u].append(pt)
+
+        def evacuate(u):
+            zp = zp_pool.tile([P, 2, 4, 256], BF16, name="zp")
+            for t, pt in enumerate(banks.pop(u)):
+                for a in range(2):
+                    k = 40 * a + 4 * (u % 10) + t
+                    affine(True, zp[:, a, t, :].rearrange("p (j m) -> p j m", j=4), pt[:, :, 64 * a:64 * a + 64],
+                           gk[:, k:k + 1], bk[:, k:k + 1])
+            planes[u] = zp
+
+        def regroup_z(u):
+            zi = zi_pool.tile([P, 2, 256, 4], BF16, name="zi", align_bytes=64)
+            nc.vector.tensor_copy(
+                out=zi[:].rearrange("p a (c i) t -> p a c t i", i=4), in_=planes.pop(u)[:].rearrange("p a t (c i) -> p a c t i", i=4)
+            )
+            grouped[u] = zi
+
+        def quantise_z(u):
+            zc = zc_pool.tile([P, 512], U32, name="zc", align_bytes=64)
+            zs = zc_pool.tile([P, 512], U8, name="zs", align_bytes=64)
+            nc.vector.quantize_mx(out=zc[:].bitcast(FP8X4), scales=zs[:], in_=grouped.pop(u)[:].rearrange("p a m t -> p (a m t)"))
+            z_codes[u] = (zc, zs)
+
+        def multiply(u):
+            mu = u % 10
+            if mu == 0:
+                for k in range(4):
+                    acc[k] = acc_pool.tile([P, 512], F32, name="acc%d" % k)
+            zc, zs = z_codes.pop(u)
+            for a in range(2):
+                g = 10 * a + mu
+                for tt in range(2):
+                    cols = slice(256 * a + P * tt, 256 * a + P * tt + P)
+                    for dst, lo, hi in ((acc[2 * tt], 0, 512), (acc[2 * tt + 1], 512, 768)):
+                        nc.tensor.matmul_mx(
+                            out=dst[:, 0:hi - lo],
+                            lhsT=zc[:, cols].bitcast(FP8X4),
+                            lhsT_scale=zs[:, cols],
+                            rhs=w_codes[g][:, lo:hi].bitcast(FP8X4),
+                            rhs_scale=w_scales[g][:, lo:hi],
+                            start=(mu == 0 and a == 0),
+                            stop=(mu == 9 and a == 1),
+                        )
 
         out_rows = out.rearrange("b (i j) n -> j (b i) n", j=8)
-        for half in range(2):
-            acc = [acc_pool.tile([P, 512], F32, name="acc%d" % k) for k in range(4)]
-            tiles = None
-            for mu in range(10):
-                if half == 0:
-                    for a in range(2):
-                        produce_w(10 * a + mu)
-                        if 2 * mu + a + 3 < 20:
-                            load_nth_w(2 * mu + a + 3)
-                zp = zp_pool.tile([P, 2, 4, 256], BF16, name="zp")
-                for t in range(4):
-                    r = 4 * mu + t
-                    if r % CHUNK_RUNS == 0:
-                        tiles = stage1(half, r // CHUNK_RUNS)
-                    pt = tp_pool.tile([P, 4, P], F32, name="tp")
-                    off = P * (r % CHUNK_RUNS)
-                    for jj in range(4):
-                        nc.tensor.transpose(out=pt[:, jj, :], in_=tiles[jj][:, off:off + P], identity=perm[:])
-                    for a in range(2):
-                        k = 40 * a + r
-                        affine(True, zp[:, a, t, :].rearrange("p (j m) -> p j m", j=4), pt[:, :, 64 * a:64 * a + 64],
-                               gk[:, k:k + 1], bk[:, k:k + 1])
-                zi = zi_pool.tile([P, 2, 256, 4], BF16, name="zi", align_bytes=64)
-                nc.vector.tensor_copy(
-                    out=zi[:].rearrange("p a (c i) t -> p a c t i", i=4), in_=zp[:].rearrange("p a t (c i) -> p a c t i", i=4)
-                )
-                zc = zc_pool.tile([P, 512], U32, name="zc", align_bytes=64)
-                zs = zc_pool.tile([P, 512], U8, name="zs", align_bytes=64)
-                nc.vector.quantize_mx(out=zc[:].bitcast(FP8X4), scales=zs[:], in_=zi[:].rearrange("p a m t -> p (a m t)"))
-                for a in range(2):
-                    g = 10 * a + mu
-                    first = mu == 0 and a == 0
-                    last = mu == 9 and a == 1
-                    for tt in range(2):
-                        cols = slice(256 * a + P * tt, 256 * a + P * tt + P)
-                        for dst, lo, hi in ((acc[2 * tt], 0, 512), (acc[2 * tt + 1], 512, 768)):
-                            nc.tensor.matmul_mx(
-                                out=dst[:, 0:hi - lo],
-                                lhsT=zc[:, cols].bitcast(FP8X4),
-                                lhsT_scale=zs[:, cols],
-                                rhs=w_codes[g][:, lo:hi].bitcast(FP8X4),
-                                rhs_scale=w_scales[g][:, lo:hi],
-                                start=first,
-                                stop=last,
-                            )
+
+        def finish(half):
             for tt in range(2):
-                o = xh_pool.tile([P, DIM], F32, name="xh")
+                o = o_pool.tile([P, DIM], F32, name="o")
                 nc.vector.tensor_tensor(out=o[:, 0:512], in0=acc[2 * tt][:], in1=b1b[:, 0:512], op=ALU.add)
                 nc.vector.tensor_tensor(out=o[:, 512:768], in0=acc[2 * tt + 1][:, 0:256], in1=b1b[:, 512:768], op=ALU.add)
                 for jl in range(2):
                     nc.sync.dma_start(out=out_rows[4 * half + 2 * tt + jl], in_=o[64 * jl:64 * jl + 64, :])
+
+        for k in range(LEAD_TILES):
+            normalise(k, 2)
+        made = LEAD_TILES
+        waiting = []
+
+        def then_quantise(job):
+            if waiting:
+                waiting.pop()()
+            if job is not None:
+                waiting.append(job)
+
+        for step in range(UNITS + 3):
+            first = HEAD_PASSES + 2 * step
+            passes = range(first, min(first + 2, PASSES))
+            if 2 <= step < UNITS + 2:
+                regroup_z(step - 2)
+                then_quantise(lambda u=step - 2: quantise_z(u))
+            for n in passes:
+                regroup_w(n, BODY_SCALAR_COLS)
+                then_quantise(lambda n=n: quantise_w(n))
+            if 1 <= step < UNITS + 1:
+                evacuate(step - 1)
+            if step >= 3:
+                multiply(step - 3)
+                if step - 3 in (9, 19):
+                    finish((step - 3) // 10)
+            if step < UNITS:
+                transposes(step)
+            target = min(32, LEAD_TILES + (8 * (step + 1) + 2) // 5)
+            while made < target:
+                normalise(made, 5 if len(passes) > 0 else 1)
+                made += 1
+            then_quantise(None)

@@ -19,7 +19,7 @@ FLOPS = 2 * B * 64 * PD * DIM
 SHIFTS = ((0, 0), (-1, -1), (-1, 1), (1, -1), (1, 1))
 PASSES = 20
 UNITS = 20
-HEAD_PASSES = 5
+HEAD_PASSES = 2
 LEAD_TILES = 5
 HEAD_SCALAR_COLS = 256
 BODY_SCALAR_COLS = 96
@@ -75,23 +75,24 @@ def tile_shiftedpatchtokenization_pa_kernel(tc, x, ln1_g, ln1_b, w1, b1, out):
                     out=w_codes[g][:, lo:hi].bitcast(FP8X4), scales=w_scales[g][:, lo:hi], in_=flat[:, 4 * lo:4 * hi]
                 )
 
-        for n in range(3):
-            load_w(n)
-        xc = consts.tile([P, C, 8, HW], BF16, name="xc")
-        xu = consts.tile([P, C, 8, HW], BF16, name="xu")
-        xd = consts.tile([P, C, 8, HW], BF16, name="xd")
-        for b in range(B):
-            nc.scalar.dma_start(
-                out=xc[b:P:8, :, :, :].rearrange("p c q w -> p c (q w)"), in_=x[b].rearrange("c (r q) w -> r c (q w)", q=8)
-            )
         graw = consts.tile([P, P], BF16, name="graw")
         braw = consts.tile([P, P], BF16, name="braw")
         nc.vector.memset(graw[:], 0.0)
         nc.vector.memset(braw[:], 0.0)
         nc.scalar.dma_start(out=graw[0:80, :], in_=ln1_g.rearrange("(r p) -> r p", p=P))
         nc.scalar.dma_start(out=braw[0:80, :], in_=ln1_b.rearrange("(r p) -> r p", p=P))
+        for n in range(HEAD_PASSES):
+            load_w(n)
+        xc = consts.tile([P, C, 8, HW], BF16, name="xc")
+        xu = consts.tile([P, C, 8, HW], BF16, name="xu")
+        xd = consts.tile([P, C, 8, HW], BF16, name="xd")
+        for b in (0, 4, 1, 5, 2, 6, 3, 7):
+            nc.scalar.dma_start(
+                out=xc[b:P:8, :, :, :].rearrange("p c q w -> p c (q w)"), in_=x[b].rearrange("c (r q) w -> r c (q w)", q=8)
+            )
+        for n in range(HEAD_PASSES, 3):
+            load_w(n)
         b1b = consts.tile([P, DIM], BF16, name="b1b")
-        nc.scalar.dma_start(out=b1b[:], in_=b1.partition_broadcast(P))
 
         eye = consts.tile([P, P], F32, name="eye")
         make_identity(nc, eye[:])
@@ -295,6 +296,8 @@ def tile_shiftedpatchtokenization_pa_kernel(tc, x, ln1_g, ln1_b, w1, b1, out):
             for n in passes:
                 regroup_w(n, BODY_SCALAR_COLS)
                 then_quantise(lambda n=n: quantise_w(n))
+            if step == 8:
+                nc.sync.dma_start(out=b1b[:], in_=b1.partition_broadcast(P))
             if 1 <= step < UNITS + 1:
                 evacuate(step - 1)
             if step >= 3:

@@ -86,9 +86,11 @@ def tile_shiftedpatchtokenization_pa_kernel(tc, x, ln1_g, ln1_b, w1, b1, out):
         xc = consts.tile([P, C, 8, HW], BF16, name="xc")
         xu = consts.tile([P, C, 8, HW], BF16, name="xu")
         xd = consts.tile([P, C, 8, HW], BF16, name="xd")
-        for b in (0, 4, 1, 5, 2, 6, 3, 7):
+        for rho in range(16):
+            first = 32 * (rho // 4) + rho % 4
             nc.scalar.dma_start(
-                out=xc[b:P:8, :, :, :].rearrange("p c q w -> p c (q w)"), in_=x[b].rearrange("c (r q) w -> r c (q w)", q=8)
+                out=xc[first:first + 29:4, :, :, :].rearrange("p c q w -> p c (q w)"),
+                in_=x[:, :, 8 * rho:8 * rho + 8, :].rearrange("b c q w -> b c (q w)"),
             )
         for n in range(HEAD_PASSES, 3):
             load_w(n)
@@ -96,28 +98,35 @@ def tile_shiftedpatchtokenization_pa_kernel(tc, x, ln1_g, ln1_b, w1, b1, out):
 
         eye = consts.tile([P, P], F32, name="eye")
         make_identity(nc, eye[:])
-        eye4 = eye[:].rearrange("p (i a b) -> p i a b", a=2, b=8)
+        eye5 = eye[:].rearrange("p (h b l a) -> p h b l a", h=4, b=8, l=2)
+        eye4 = eye[:].rearrange("p (h b r) -> p h b r", h=4, b=8)
         perm = consts.tile([P, P], F32, name="perm")
         nc.vector.tensor_copy(
-            out=perm[:].rearrange("p (a b i) -> p a b i", a=2, b=8), in_=eye[:].rearrange("p (i a b) -> p a b i", a=2, b=8)
+            out=perm[:].rearrange("p (a b h l) -> p a b h l", a=2, b=8, h=4), in_=eye[:].rearrange("p (h b l a) -> p a b h l", h=4, b=8, l=2)
         )
         rot_up = consts.tile([P, P], BF16, name="rot_up")
         rot_dn = consts.tile([P, P], BF16, name="rot_dn")
         nc.vector.memset(rot_up[:], 0.0)
         nc.vector.memset(rot_dn[:], 0.0)
-        nc.vector.tensor_copy(out=rot_up[:, 8:P], in_=eye[:, 0:120])
-        nc.vector.tensor_copy(out=rot_dn[:, 0:120], in_=eye[:, 8:P])
-        tok2 = consts.tile([P, 8, 8], F32, name="tok2")
-        tok4 = consts.tile([P, 8, 8], F32, name="tok4")
-        nc.vector.tensor_add(out=tok2[:], in0=eye4[:, :, 0, :], in1=eye4[:, :, 1, :])
+        up4 = rot_up[:].rearrange("p (h b r) -> p h b r", h=4, b=8)
+        dn4 = rot_dn[:].rearrange("p (h b r) -> p h b r", h=4, b=8)
+        nc.vector.tensor_copy(out=up4[:, :, :, 1:4], in_=eye4[:, :, :, 0:3])
+        nc.vector.tensor_copy(out=up4[:, 1:4, :, 0], in_=eye4[:, 0:3, :, 3])
+        nc.vector.tensor_copy(out=dn4[:, :, :, 0:3], in_=eye4[:, :, :, 1:4])
+        nc.vector.tensor_copy(out=dn4[:, 0:3, :, 3], in_=eye4[:, 1:4, :, 0])
+        tok2 = consts.tile([P, 4, 8, 2], F32, name="tok2")
+        tok4 = consts.tile([P, 4, 8, 2], F32, name="tok4")
+        nc.vector.tensor_add(out=tok2[:], in0=eye5[:, :, :, :, 0], in1=eye5[:, :, :, :, 1])
         nc.vector.tensor_copy(out=tok4[:], in_=tok2[:])
-        nc.vector.tensor_add(out=tok4[:, 1:8, :], in0=tok4[:, 1:8, :], in1=eye4[:, 0:7, 1, :])
-        nc.vector.tensor_add(out=tok4[:, 0:7, :], in0=tok4[:, 0:7, :], in1=eye4[:, 1:8, 0, :])
+        nc.vector.tensor_add(out=tok4[:, :, :, 1], in0=tok4[:, :, :, 1], in1=eye5[:, :, :, 0, 1])
+        nc.vector.tensor_add(out=tok4[:, 1:4, :, 0], in0=tok4[:, 1:4, :, 0], in1=eye5[:, 0:3, :, 1, 1])
+        nc.vector.tensor_add(out=tok4[:, :, :, 0], in0=tok4[:, :, :, 0], in1=eye5[:, :, :, 1, 0])
+        nc.vector.tensor_add(out=tok4[:, 0:3, :, 1], in0=tok4[:, 0:3, :, 1], in1=eye5[:, 1:4, :, 0, 0])
         rows4 = consts.tile([P, P], F32, name="rows4")
         rows2 = consts.tile([P, P], F32, name="rows2")
         for a in range(2):
-            nc.vector.tensor_copy(out=rows4[:].rearrange("p (i a b) -> p i a b", a=2, b=8)[:, :, a, :], in_=tok4[:])
-            nc.vector.tensor_copy(out=rows2[:].rearrange("p (i a b) -> p i a b", a=2, b=8)[:, :, a, :], in_=tok2[:])
+            nc.vector.tensor_copy(out=rows4[:].rearrange("p (h b l a) -> p h b l a", h=4, b=8, l=2)[:, :, :, :, a], in_=tok4[:])
+            nc.vector.tensor_copy(out=rows2[:].rearrange("p (h b l a) -> p h b l a", h=4, b=8, l=2)[:, :, :, :, a], in_=tok2[:])
         padded = consts.tile([P, 4, 18], F32, name="padded")
         nc.vector.memset(padded[:], 0.0)
 
@@ -251,9 +260,9 @@ def tile_shiftedpatchtokenization_pa_kernel(tc, x, ln1_g, ln1_b, w1, b1, out):
                 for k in range(4):
                     acc[k] = acc_pool.tile([P, 512], F32, name="acc%d" % k)
             zc, zs = z_codes.pop(u)
-            for a in range(2):
-                g = 10 * a + mu
-                for tt in range(2):
+            for tt in range(2):
+                for a in range(2):
+                    g = 10 * a + mu
                     cols = slice(256 * a + P * tt, 256 * a + P * tt + P)
                     for dst, lo, hi in ((acc[2 * tt], 0, 512), (acc[2 * tt + 1], 512, 768)):
                         nc.tensor.matmul_mx(
@@ -288,8 +297,7 @@ def tile_shiftedpatchtokenization_pa_kernel(tc, x, ln1_g, ln1_b, w1, b1, out):
                 waiting.append(job)
 
         for step in range(UNITS + 3):
-            first = HEAD_PASSES + 2 * step
-            passes = range(first, min(first + 2, PASSES))
+            passes = range(min(HEAD_PASSES + (3 * step + 1) // 2, PASSES), min(HEAD_PASSES + (3 * step + 4) // 2, PASSES))
             if 2 <= step < UNITS + 2:
                 regroup_z(step - 2)
                 then_quantise(lambda u=step - 2: quantise_z(u))
@@ -308,6 +316,6 @@ def tile_shiftedpatchtokenization_pa_kernel(tc, x, ln1_g, ln1_b, w1, b1, out):
                 transposes(step)
             target = min(32, LEAD_TILES + (8 * (step + 1) + 2) // 5)
             while made < target:
-                normalise(made, 5 if len(passes) > 0 else 1)
+                normalise(made, 1 + 2 * len(passes))
                 made += 1
             then_quantise(None)

@@ -316,6 +316,6 @@ def tile_shiftedpatchtokenization_pa_kernel(tc, x, ln1_g, ln1_b, w1, b1, out):
                 transposes(step)
             target = min(32, LEAD_TILES + (8 * (step + 1) + 2) // 5)
             while made < target:
-                normalise(made, 1 + 2 * len(passes))
+                normalise(made, 2 * len(passes))
                 made += 1
             then_quantise(None)

@@ -10,6 +10,7 @@ U8 = mybir.dt.uint8
 FP8X4 = mybir.dt.float8_e4m3fn_x4
 ALU = mybir.AluOpType
 ACT = mybir.ActivationFunctionType
+AX = mybir.AxisListType
 
 P = 128
 B, C, HW, DIM = 8, 8, 128, 768
@@ -86,12 +87,13 @@ def tile_shiftedpatchtokenization_pa_kernel(tc, x, ln1_g, ln1_b, w1, b1, out):
         xc = consts.tile([P, C, 8, HW], BF16, name="xc")
         xu = consts.tile([P, C, 8, HW], BF16, name="xu")
         xd = consts.tile([P, C, 8, HW], BF16, name="xd")
-        for rho in range(16):
-            first = 32 * (rho // 4) + rho % 4
-            nc.scalar.dma_start(
-                out=xc[first:first + 29:4, :, :, :].rearrange("p c q w -> p c (q w)"),
-                in_=x[:, :, 8 * rho:8 * rho + 8, :].rearrange("b c q w -> b c (q w)"),
-            )
+        for c0 in (0, 4):
+            for rho in range(16):
+                first = 32 * (rho // 4) + rho % 4
+                nc.scalar.dma_start(
+                    out=xc[first:first + 29:4, c0:c0 + 4, :, :].rearrange("p c q w -> p c (q w)"),
+                    in_=x[:, c0:c0 + 4, 8 * rho:8 * rho + 8, :].rearrange("b c q w -> b c (q w)"),
+                )
         for n in range(HEAD_PASSES, 3):
             load_w(n)
         b1b = consts.tile([P, DIM], BF16, name="b1b")
@@ -145,9 +147,10 @@ def tile_shiftedpatchtokenization_pa_kernel(tc, x, ln1_g, ln1_b, w1, b1, out):
             nc.vector.tensor_copy(out=dst[:], in_=pt[:, 0, 0:80])
         quantise_w(HEAD_PASSES - 1)
 
-        st6 = consts.tile([P, 16, 6], F32, name="st6")
-        for j in range(16):
-            nc.vector.bn_stats(out=st6[:, j, :], in_=xc[:, :, :, 8 * j:8 * j + 8])
+        st6 = consts.tile([P, 16, 2, 6], F32, name="st6")
+        for h in range(2):
+            for j in range(16):
+                nc.vector.bn_stats(out=st6[:, j, h, :], in_=xc[:, 4 * h:4 * h + 4, :, 8 * j:8 * j + 8])
         xc_flat = xc[:].rearrange("p c q w -> p (c q w)")
         for m in range(C):
             for rot, dst in ((rot_up, xu), (rot_dn, xd)):
@@ -156,16 +159,16 @@ def tile_shiftedpatchtokenization_pa_kernel(tc, x, ln1_g, ln1_b, w1, b1, out):
                     lo = 1024 * m + 512 * h
                     nc.tensor.matmul(out=ps[:, 512 * h:512 * h + 512], lhsT=rot[:], rhs=xc_flat[:, lo:lo + 512], start=True, stop=True)
                 nc.scalar.copy(out=dst[:].rearrange("p c q w -> p (c q w)")[:, 1024 * m:1024 * m + 1024], in_=ps[:])
-        halves = st6[:].rearrange("p j (h k) -> p j h k", h=2)
+        groups = st6[:].rearrange("p j h (e k) -> p j (h e) k", e=2)
         cells = consts.tile([P, 2, 16], F32, name="cells")
-        sqm = consts.tile([P, 16, 2], F32, name="sqm")
+        sqm = consts.tile([P, 16, 4], F32, name="sqm")
         s2 = consts.tile([P, 16], F32, name="s2")
         m2 = consts.tile([P, 16], F32, name="m2")
-        nc.vector.tensor_add(out=cells[:, 0, :], in0=halves[:, :, 0, 1], in1=halves[:, :, 1, 1])
-        nc.vector.tensor_mul(out=sqm[:], in0=halves[:, :, :, 1], in1=halves[:, :, :, 1])
-        nc.vector.tensor_add(out=m2[:], in0=halves[:, :, 0, 2], in1=halves[:, :, 1, 2])
-        nc.vector.tensor_add(out=s2[:], in0=sqm[:, :, 0], in1=sqm[:, :, 1])
-        nc.vector.scalar_tensor_tensor(out=cells[:, 1, :], in0=s2[:], scalar=256.0, in1=m2[:], op0=ALU.mult, op1=ALU.add)
+        nc.vector.tensor_reduce(out=cells[:, 0, :], in_=groups[:, :, :, 1], axis=AX.X, op=ALU.add)
+        nc.vector.tensor_mul(out=sqm[:], in0=groups[:, :, :, 1], in1=groups[:, :, :, 1])
+        nc.vector.tensor_reduce(out=m2[:], in_=groups[:, :, :, 2], axis=AX.X, op=ALU.add)
+        nc.vector.tensor_reduce(out=s2[:], in_=sqm[:], axis=AX.X, op=ALU.add)
+        nc.vector.scalar_tensor_tensor(out=cells[:, 1, :], in0=s2[:], scalar=128.0, in1=m2[:], op0=ALU.mult, op1=ALU.add)
         st = tp_pool.tile([P, 4, P], F32, name="tp")
         nc.tensor.matmul(out=st[:, 0, 0:32], lhsT=rows4[:], rhs=cells[:].rearrange("p s j -> p (s j)"), start=True, stop=True)
         nc.tensor.matmul(out=st[:, 0, 32:64], lhsT=rows2[:], rhs=cells[:].rearrange("p s j -> p (s j)"), start=True, stop=True)
@@ -181,7 +184,7 @@ def tile_shiftedpatchtokenization_pa_kernel(tc, x, ln1_g, ln1_b, w1, b1, out):
         for nm in ("mean", "msq", "var", "std", "r0", "nt", "rstd", "nmr"):
             small[nm] = consts.tile([P, 8], F32, name=nm)
         mean, msq, var, std, r0, nt, rstd, nmr = (small[nm] for nm in ("mean", "msq", "var", "std", "r0", "nt", "rstd", "nmr"))
-        nc.vector.tensor_scalar_mul(out=mean[:], in0=tot[:, 0, :], scalar1=256.0 / PD)
+        nc.vector.tensor_scalar_mul(out=mean[:], in0=tot[:, 0, :], scalar1=128.0 / PD)
         nc.vector.tensor_mul(out=msq[:], in0=mean[:], in1=mean[:])
         nc.vector.scalar_tensor_tensor(out=var[:], in0=tot[:, 1, :], scalar=1.0 / PD, in1=msq[:], op0=ALU.mult, op1=ALU.subtract)
         nc.vector.tensor_scalar(out=var[:], in0=var[:], scalar1=0.0, scalar2=EPS, op0=ALU.max, op1=ALU.add)
@@ -316,6 +319,6 @@ def tile_shiftedpatchtokenization_pa_kernel(tc, x, ln1_g, ln1_b, w1, b1, out):
                 transposes(step)
             target = min(32, LEAD_TILES + (8 * (step + 1) + 2) // 5)
             while made < target:
-                normalise(made, 2 * len(passes))
+                normalise(made, 1 + 2 * len(passes))
                 made += 1
             then_quantise(None)

@@ -90,7 +90,7 @@ def tile_shiftedpatchtokenization_pa_kernel(tc, x, ln1_g, ln1_b, w1, b1, out):
         for c0 in (0, 4):
             for rho in range(16):
                 first = 32 * (rho // 4) + rho % 4
-                nc.scalar.dma_start(
+                nc.sync.dma_start(
                     out=xc[first:first + 29:4, c0:c0 + 4, :, :].rearrange("p c q w -> p c (q w)"),
                     in_=x[:, c0:c0 + 4, 8 * rho:8 * rho + 8, :].rearrange("b c q w -> b c (q w)"),
                 )

@@ -18,10 +18,13 @@ PD = 10240
 EPS = 1e-5
 FLOPS = 2 * B * 64 * PD * DIM
 SHIFTS = ((0, 0), (-1, -1), (-1, 1), (1, -1), (1, 1))
-PASSES = 20
+PASSES = PD // 512
 UNITS = 20
+STRIPS = 32
+RUNS_PER_STRIP = 10
+W_LOADS_AHEAD = 3
 HEAD_PASSES = 2
-LEAD_TILES = 5
+LEAD_STRIPS = 5
 HEAD_SCALAR_COLS = 256
 BODY_SCALAR_COLS = 96
 
@@ -31,7 +34,7 @@ def tile_shiftedpatchtokenization_pa_kernel(tc, x, ln1_g, ln1_b, w1, b1, out):
     with ExitStack() as ctx:
         ctx.enter_context(tc.manual_schedule())
         consts = ctx.enter_context(tc.tile_pool(name="consts", bufs=1))
-        wraw_pool = ctx.enter_context(tc.tile_pool(name="wraw", bufs=3))
+        wraw_pool = ctx.enter_context(tc.tile_pool(name="wraw", bufs=W_LOADS_AHEAD))
         wi_pool = ctx.enter_context(tc.tile_pool(name="wi", bufs=2))
         xh_pool = ctx.enter_context(tc.tile_pool(name="xh", bufs=8))
         zp_pool = ctx.enter_context(tc.tile_pool(name="zp", bufs=2))
@@ -46,31 +49,31 @@ def tile_shiftedpatchtokenization_pa_kernel(tc, x, ln1_g, ln1_b, w1, b1, out):
         w_raw = {}
         w_grouped = {}
 
-        def nth_pass(n):
-            return 10 * (n % 2) + n // 2
+        def nth_pass(nth):
+            return 10 * (nth % 2) + nth // 2
 
-        def load_w(n):
-            if n < PASSES:
-                g = nth_pass(n)
+        def load_w(nth):
+            if nth < PASSES:
+                g = nth_pass(nth)
                 wr = wraw_pool.tile([P, 4, DIM], BF16, name="wr")
                 nc.sync.dma_start(out=wr[:], in_=w1[512 * g:512 * g + 512, :].rearrange("(t p) n -> p t n", p=P))
-                w_raw[n] = wr
+                w_raw[nth] = wr
 
         def regroup4(copy, dst, src):
             copy(out=dst.rearrange("p (c i) t -> p c t i", i=4), in_=src.rearrange("p t (c i) -> p c t i", i=4))
 
-        def regroup_w(n, scalar_cols):
-            wr = w_raw.pop(n)
+        def regroup_w(nth, scalar_cols):
+            wr = w_raw.pop(nth)
             wi = wi_pool.tile([P, DIM, 4], BF16, name="wi", align_bytes=64)
             cut = DIM - scalar_cols
             regroup4(nc.scalar.copy, wi[:, cut:DIM, :], wr[:, :, cut:DIM])
             regroup4(nc.vector.tensor_copy, wi[:, 0:cut, :], wr[:, :, 0:cut])
-            w_grouped[n] = wi
-            load_w(n + 3)
+            w_grouped[nth] = wi
+            load_w(nth + W_LOADS_AHEAD)
 
-        def quantise_w(n):
-            g = nth_pass(n)
-            flat = w_grouped.pop(n)[:].rearrange("p n t -> p (n t)")
+        def quantise_w(nth):
+            g = nth_pass(nth)
+            flat = w_grouped.pop(nth)[:].rearrange("p n t -> p (n t)")
             for lo, hi in ((0, 512), (512, 768)):
                 nc.vector.quantize_mx(
                     out=w_codes[g][:, lo:hi].bitcast(FP8X4), scales=w_scales[g][:, lo:hi], in_=flat[:, 4 * lo:4 * hi]
@@ -82,8 +85,11 @@ def tile_shiftedpatchtokenization_pa_kernel(tc, x, ln1_g, ln1_b, w1, b1, out):
         nc.vector.memset(braw[:], 0.0)
         nc.scalar.dma_start(out=graw[0:80, :], in_=ln1_g.rearrange("(r p) -> r p", p=P))
         nc.scalar.dma_start(out=braw[0:80, :], in_=ln1_b.rearrange("(r p) -> r p", p=P))
-        for n in range(HEAD_PASSES):
-            load_w(n)
+        warm = consts.tile([P, 1], F32, name="warm")
+        nc.vector.memset(warm[:], 1.0)
+        nc.scalar.sqrt(out=warm[:], in_=warm[:])
+        for nth in range(HEAD_PASSES):
+            load_w(nth)
         xc = consts.tile([P, C, 8, HW], BF16, name="xc")
         xu = consts.tile([P, C, 8, HW], BF16, name="xu")
         xd = consts.tile([P, C, 8, HW], BF16, name="xd")
@@ -94,8 +100,8 @@ def tile_shiftedpatchtokenization_pa_kernel(tc, x, ln1_g, ln1_b, w1, b1, out):
                     out=xc[first:first + 29:4, c0:c0 + 4, :, :].rearrange("p c q w -> p c (q w)"),
                     in_=x[:, c0:c0 + 4, 8 * rho:8 * rho + 8, :].rearrange("b c q w -> b c (q w)"),
                 )
-        for n in range(HEAD_PASSES, 3):
-            load_w(n)
+        for nth in range(HEAD_PASSES, W_LOADS_AHEAD):
+            load_w(nth)
         b1b = consts.tile([P, DIM], BF16, name="b1b")
 
         eye = consts.tile([P, P], F32, name="eye")
@@ -133,9 +139,9 @@ def tile_shiftedpatchtokenization_pa_kernel(tc, x, ln1_g, ln1_b, w1, b1, out):
         nc.vector.memset(padded[:], 0.0)
 
         regroup_w(0, HEAD_SCALAR_COLS)
-        for n in range(1, HEAD_PASSES):
-            regroup_w(n, HEAD_SCALAR_COLS)
-            quantise_w(n - 1)
+        for nth in range(1, HEAD_PASSES):
+            regroup_w(nth, HEAD_SCALAR_COLS)
+            quantise_w(nth - 1)
 
         gk = consts.tile([P, 80], F32, name="gk")
         bk = consts.tile([P, 80], F32, name="bk")
@@ -148,18 +154,22 @@ def tile_shiftedpatchtokenization_pa_kernel(tc, x, ln1_g, ln1_b, w1, b1, out):
         quantise_w(HEAD_PASSES - 1)
 
         st6 = consts.tile([P, 16, 2, 6], F32, name="st6")
-        for h in range(2):
-            for j in range(16):
-                nc.vector.bn_stats(out=st6[:, j, h, :], in_=xc[:, 4 * h:4 * h + 4, :, 8 * j:8 * j + 8])
+        for c_half in range(2):
+            for cell_col in range(16):
+                nc.vector.bn_stats(
+                    out=st6[:, cell_col, c_half, :], in_=xc[:, 4 * c_half:4 * c_half + 4, :, 8 * cell_col:8 * cell_col + 8]
+                )
         xc_flat = xc[:].rearrange("p c q w -> p (c q w)")
-        for m in range(C):
+        for c in range(C):
             for rot, dst in ((rot_up, xu), (rot_dn, xd)):
                 ps = tp_pool.tile([P, 1024], BF16, name="tp")
-                for h in range(2):
-                    lo = 1024 * m + 512 * h
-                    nc.tensor.matmul(out=ps[:, 512 * h:512 * h + 512], lhsT=rot[:], rhs=xc_flat[:, lo:lo + 512], start=True, stop=True)
-                nc.scalar.copy(out=dst[:].rearrange("p c q w -> p (c q w)")[:, 1024 * m:1024 * m + 1024], in_=ps[:])
-        groups = st6[:].rearrange("p j h (e k) -> p j (h e) k", e=2)
+                for bank_half in range(2):
+                    lo = 1024 * c + 512 * bank_half
+                    nc.tensor.matmul(
+                        out=ps[:, 512 * bank_half:512 * bank_half + 512], lhsT=rot[:], rhs=xc_flat[:, lo:lo + 512], start=True, stop=True
+                    )
+                nc.scalar.copy(out=dst[:].rearrange("p c q w -> p (c q w)")[:, 1024 * c:1024 * c + 1024], in_=ps[:])
+        groups = st6[:].rearrange("p d f (e v) -> p d (f e) v", e=2)
         cells = consts.tile([P, 2, 16], F32, name="cells")
         sqm = consts.tile([P, 16, 4], F32, name="sqm")
         s2 = consts.tile([P, 16], F32, name="s2")
@@ -170,9 +180,9 @@ def tile_shiftedpatchtokenization_pa_kernel(tc, x, ln1_g, ln1_b, w1, b1, out):
         nc.vector.tensor_reduce(out=s2[:], in_=sqm[:], axis=AX.X, op=ALU.add)
         nc.vector.scalar_tensor_tensor(out=cells[:, 1, :], in0=s2[:], scalar=128.0, in1=m2[:], op0=ALU.mult, op1=ALU.add)
         st = tp_pool.tile([P, 4, P], F32, name="tp")
-        nc.tensor.matmul(out=st[:, 0, 0:32], lhsT=rows4[:], rhs=cells[:].rearrange("p s j -> p (s j)"), start=True, stop=True)
-        nc.tensor.matmul(out=st[:, 0, 32:64], lhsT=rows2[:], rhs=cells[:].rearrange("p s j -> p (s j)"), start=True, stop=True)
-        nc.vector.tensor_copy(out=padded[:, :, 1:17], in_=st[:, 0, 0:64].rearrange("p (k j) -> p k j", j=16))
+        nc.tensor.matmul(out=st[:, 0, 0:32], lhsT=rows4[:], rhs=cells[:].rearrange("p f d -> p (f d)"), start=True, stop=True)
+        nc.tensor.matmul(out=st[:, 0, 32:64], lhsT=rows2[:], rhs=cells[:].rearrange("p f d -> p (f d)"), start=True, stop=True)
+        nc.vector.tensor_copy(out=padded[:, :, 1:17], in_=st[:, 0, 0:64].rearrange("p (f d) -> p f d", d=16))
         pairs = consts.tile([P, 2, 9], F32, name="pairs")
         inner = consts.tile([P, 2, 8], F32, name="inner")
         tot = consts.tile([P, 2, 8], F32, name="tot")
@@ -202,12 +212,12 @@ def tile_shiftedpatchtokenization_pa_kernel(tc, x, ln1_g, ln1_b, w1, b1, out):
             else:
                 nc.vector.tensor_scalar(out=dst, in0=src, scalar1=scale, scalar2=bias, op0=ALU.mult, op1=ALU.add)
 
-        xh_tiles = {}
+        strips = {}
 
-        def normalise(k, n_scalar):
-            j = 4 * (k // 16) + k % 4
-            chunk = (k % 16) // 4
-            xh = xh_pool.tile([P, 1280], F32, name="xh")
+        def normalise(strip, n_scalar):
+            j = 4 * (strip // 16) + strip % 4
+            row_pair = (strip % 16) // 4
+            xh = xh_pool.tile([P, 128 * RUNS_PER_STRIP], F32, name="xh")
             view = xh[:].rearrange("p (q e s c) -> p q e s c", q=2, e=16, s=5)
             for s, (di, dj) in enumerate(SHIFTS):
                 source = (xu, xc, xd)[di + 1]
@@ -215,23 +225,25 @@ def tile_shiftedpatchtokenization_pa_kernel(tc, x, ln1_g, ln1_b, w1, b1, out):
                 lo = 8 if col0 < 0 else 0
                 hi = 8 if col0 + 16 > HW else 16
                 on_scalar = s >= 5 - n_scalar
-                for ch in range(2):
-                    src = source[:, 4 * ch:4 * ch + 4, 2 * chunk:2 * chunk + 2, col0 + lo:col0 + hi].rearrange("p c q e -> p q e c")
-                    affine(on_scalar, view[:, :, lo:hi, s, 4 * ch:4 * ch + 4], src, rstd[:, j:j + 1], nmr[:, j:j + 1])
+                for c4 in range(2):
+                    src = source[:, 4 * c4:4 * c4 + 4, 2 * row_pair:2 * row_pair + 2, col0 + lo:col0 + hi].rearrange("p c q e -> p q e c")
+                    affine(on_scalar, view[:, :, lo:hi, s, 4 * c4:4 * c4 + 4], src, rstd[:, j:j + 1], nmr[:, j:j + 1])
                     if hi - lo < 16:
-                        affine(on_scalar, view[:, :, 8 - lo:24 - hi, s, 4 * ch:4 * ch + 4], src, 0.0, nmr[:, j:j + 1])
-            xh_tiles[k] = xh
+                        affine(on_scalar, view[:, :, 8 - lo:24 - hi, s, 4 * c4:4 * c4 + 4], src, 0.0, nmr[:, j:j + 1])
+            strips[strip] = xh
 
         banks, planes, grouped, z_codes, acc = {}, {}, {}, {}, {}
 
         def transposes(u):
             banks[u] = []
             for t in range(4):
-                run = 4 * u + t
+                nth_run = 4 * u + t
                 pt = tp_pool.tile([P, 4, P], F32, name="tp")
                 for jj in range(4):
                     nc.tensor.transpose(
-                        out=pt[:, jj, :], in_=xh_tiles[4 * (run // 10) + jj][:, P * (run % 10):P * (run % 10) + P], identity=perm[:]
+                        out=pt[:, jj, :],
+                        in_=strips[4 * (nth_run // RUNS_PER_STRIP) + jj][:, P * (nth_run % RUNS_PER_STRIP):P * (nth_run % RUNS_PER_STRIP) + P],
+                        identity=perm[:],
                     )
                 banks[u].append(pt)
 
@@ -239,9 +251,9 @@ def tile_shiftedpatchtokenization_pa_kernel(tc, x, ln1_g, ln1_b, w1, b1, out):
             zp = zp_pool.tile([P, 2, 4, 256], BF16, name="zp")
             for t, pt in enumerate(banks.pop(u)):
                 for a in range(2):
-                    k = 40 * a + 4 * (u % 10) + t
+                    col = 40 * a + 4 * (u % 10) + t
                     affine(True, zp[:, a, t, :].rearrange("p (j m) -> p j m", j=4), pt[:, :, 64 * a:64 * a + 64],
-                           gk[:, k:k + 1], bk[:, k:k + 1])
+                           gk[:, col:col + 1], bk[:, col:col + 1])
             planes[u] = zp
 
         def regroup_z(u):
@@ -260,8 +272,8 @@ def tile_shiftedpatchtokenization_pa_kernel(tc, x, ln1_g, ln1_b, w1, b1, out):
         def multiply(u):
             mu = u % 10
             if mu == 0:
-                for k in range(4):
-                    acc[k] = acc_pool.tile([P, 512], F32, name="acc%d" % k)
+                for bank in range(4):
+                    acc[bank] = acc_pool.tile([P, 512], F32, name="acc%d" % bank)
             zc, zs = z_codes.pop(u)
             for tt in range(2):
                 for a in range(2):
@@ -288,9 +300,9 @@ def tile_shiftedpatchtokenization_pa_kernel(tc, x, ln1_g, ln1_b, w1, b1, out):
                 for jl in range(2):
                     nc.sync.dma_start(out=out_rows[4 * half + 2 * tt + jl], in_=o[64 * jl:64 * jl + 64, :])
 
-        for k in range(LEAD_TILES):
-            normalise(k, 2)
-        made = LEAD_TILES
+        for strip in range(LEAD_STRIPS):
+            normalise(strip, 2)
+        made = LEAD_STRIPS
         waiting = []
 
         def then_quantise(job):
@@ -304,9 +316,9 @@ def tile_shiftedpatchtokenization_pa_kernel(tc, x, ln1_g, ln1_b, w1, b1, out):
             if 2 <= step < UNITS + 2:
                 regroup_z(step - 2)
                 then_quantise(lambda u=step - 2: quantise_z(u))
-            for n in passes:
-                regroup_w(n, BODY_SCALAR_COLS)
-                then_quantise(lambda n=n: quantise_w(n))
+            for nth in passes:
+                regroup_w(nth, BODY_SCALAR_COLS)
+                then_quantise(lambda nth=nth: quantise_w(nth))
             if step == 8:
                 nc.sync.dma_start(out=b1b[:], in_=b1.partition_broadcast(P))
             if 1 <= step < UNITS + 1:
@@ -317,7 +329,7 @@ def tile_shiftedpatchtokenization_pa_kernel(tc, x, ln1_g, ln1_b, w1, b1, out):
                     finish((step - 3) // 10)
             if step < UNITS:
                 transposes(step)
-            target = min(32, LEAD_TILES + (8 * (step + 1) + 2) // 5)
+            target = min(STRIPS, LEAD_STRIPS + (8 * (step + 1) + 2) // 5)
             while made < target:
                 normalise(made, 1 + 2 * len(passes))
                 made += 1

from contextlib import ExitStack

import concourse.mybir as mybir
from concourse.masks import make_identity

F32 = mybir.dt.float32
BF16 = mybir.dt.bfloat16
U32 = mybir.dt.uint32
U8 = mybir.dt.uint8
FP8X4 = mybir.dt.float8_e4m3fn_x4
ALU = mybir.AluOpType
ACT = mybir.ActivationFunctionType
AX = mybir.AxisListType

P = 128
B, C, HW, DIM = 8, 8, 128, 768
PD = 10240
EPS = 1e-5
FLOPS = 2 * B * 64 * PD * DIM
SHIFTS = ((0, 0), (-1, -1), (-1, 1), (1, -1), (1, 1))
PASSES = PD // 512
UNITS = 20
STRIPS = 32
RUNS_PER_STRIP = 10
W_LOADS_AHEAD = 3
HEAD_PASSES = 2
LEAD_STRIPS = 5
HEAD_SCALAR_COLS = 256
BODY_SCALAR_COLS = 96


def tile_shiftedpatchtokenization_pa_kernel(tc, x, ln1_g, ln1_b, w1, b1, out):
    nc = tc.nc
    with ExitStack() as ctx:
        ctx.enter_context(tc.manual_schedule())
        consts = ctx.enter_context(tc.tile_pool(name="consts", bufs=1))
        wraw_pool = ctx.enter_context(tc.tile_pool(name="wraw", bufs=W_LOADS_AHEAD))
        wi_pool = ctx.enter_context(tc.tile_pool(name="wi", bufs=2))
        xh_pool = ctx.enter_context(tc.tile_pool(name="xh", bufs=8))
        zp_pool = ctx.enter_context(tc.tile_pool(name="zp", bufs=2))
        zi_pool = ctx.enter_context(tc.tile_pool(name="zi", bufs=2))
        zc_pool = ctx.enter_context(tc.tile_pool(name="zc", bufs=3))
        o_pool = ctx.enter_context(tc.tile_pool(name="o", bufs=2))
        acc_pool = ctx.enter_context(tc.psum_pool(name="acc", bufs=1))
        tp_pool = ctx.enter_context(tc.psum_pool(name="tp", bufs=4))

        w_codes = [consts.tile([P, DIM], U32, name="wc%d" % g, align_bytes=64) for g in range(PASSES)]
        w_scales = [consts.tile([P, DIM], U8, name="ws%d" % g, align_bytes=64) for g in range(PASSES)]
        w_raw = {}
        w_grouped = {}

        def nth_pass(nth):
            return 10 * (nth % 2) + nth // 2

        def load_w(nth):
            if nth < PASSES:
                g = nth_pass(nth)
                wr = wraw_pool.tile([P, 4, DIM], BF16, name="wr")
                nc.sync.dma_start(out=wr[:], in_=w1[512 * g:512 * g + 512, :].rearrange("(t p) n -> p t n", p=P))
                w_raw[nth] = wr

        def regroup4(copy, dst, src):
            copy(out=dst.rearrange("p (c i) t -> p c t i", i=4), in_=src.rearrange("p t (c i) -> p c t i", i=4))

        def regroup_w(nth, scalar_cols):
            wr = w_raw.pop(nth)
            wi = wi_pool.tile([P, DIM, 4], BF16, name="wi", align_bytes=64)
            cut = DIM - scalar_cols
            regroup4(nc.scalar.copy, wi[:, cut:DIM, :], wr[:, :, cut:DIM])
            regroup4(nc.vector.tensor_copy, wi[:, 0:cut, :], wr[:, :, 0:cut])
            w_grouped[nth] = wi
            load_w(nth + W_LOADS_AHEAD)

        def quantise_w(nth):
            g = nth_pass(nth)
            flat = w_grouped.pop(nth)[:].rearrange("p n t -> p (n t)")
            for lo, hi in ((0, 512), (512, 768)):
                nc.vector.quantize_mx(
                    out=w_codes[g][:, lo:hi].bitcast(FP8X4), scales=w_scales[g][:, lo:hi], in_=flat[:, 4 * lo:4 * hi]
                )

        graw = consts.tile([P, P], BF16, name="graw")
        braw = consts.tile([P, P], BF16, name="braw")
        nc.vector.memset(graw[:], 0.0)
        nc.vector.memset(braw[:], 0.0)
        nc.scalar.dma_start(out=graw[0:80, :], in_=ln1_g.rearrange("(r p) -> r p", p=P))
        nc.scalar.dma_start(out=braw[0:80, :], in_=ln1_b.rearrange("(r p) -> r p", p=P))
        warm = consts.tile([P, 1], F32, name="warm")
        nc.vector.memset(warm[:], 1.0)
        nc.scalar.sqrt(out=warm[:], in_=warm[:])
        for nth in range(HEAD_PASSES):
            load_w(nth)
        xc = consts.tile([P, C, 8, HW], BF16, name="xc")
        xu = consts.tile([P, C, 8, HW], BF16, name="xu")
        xd = consts.tile([P, C, 8, HW], BF16, name="xd")
        for c0 in (0, 4):
            for rho in range(16):
                first = 32 * (rho // 4) + rho % 4
                nc.sync.dma_start(
                    out=xc[first:first + 29:4, c0:c0 + 4, :, :].rearrange("p c q w -> p c (q w)"),
                    in_=x[:, c0:c0 + 4, 8 * rho:8 * rho + 8, :].rearrange("b c q w -> b c (q w)"),
                )
        for nth in range(HEAD_PASSES, W_LOADS_AHEAD):
            load_w(nth)
        b1b = consts.tile([P, DIM], BF16, name="b1b")

        eye = consts.tile([P, P], F32, name="eye")
        make_identity(nc, eye[:])
        eye5 = eye[:].rearrange("p (h b l a) -> p h b l a", h=4, b=8, l=2)
        eye4 = eye[:].rearrange("p (h b r) -> p h b r", h=4, b=8)
        perm = consts.tile([P, P], F32, name="perm")
        nc.vector.tensor_copy(
            out=perm[:].rearrange("p (a b h l) -> p a b h l", a=2, b=8, h=4), in_=eye[:].rearrange("p (h b l a) -> p a b h l", h=4, b=8, l=2)
        )
        rot_up = consts.tile([P, P], BF16, name="rot_up")
        rot_dn = consts.tile([P, P], BF16, name="rot_dn")
        nc.vector.memset(rot_up[:], 0.0)
        nc.vector.memset(rot_dn[:], 0.0)
        up4 = rot_up[:].rearrange("p (h b r) -> p h b r", h=4, b=8)
        dn4 = rot_dn[:].rearrange("p (h b r) -> p h b r", h=4, b=8)
        nc.vector.tensor_copy(out=up4[:, :, :, 1:4], in_=eye4[:, :, :, 0:3])
        nc.vector.tensor_copy(out=up4[:, 1:4, :, 0], in_=eye4[:, 0:3, :, 3])
        nc.vector.tensor_copy(out=dn4[:, :, :, 0:3], in_=eye4[:, :, :, 1:4])
        nc.vector.tensor_copy(out=dn4[:, 0:3, :, 3], in_=eye4[:, 1:4, :, 0])
        tok2 = consts.tile([P, 4, 8, 2], F32, name="tok2")
        tok4 = consts.tile([P, 4, 8, 2], F32, name="tok4")
        nc.vector.tensor_add(out=tok2[:], in0=eye5[:, :, :, :, 0], in1=eye5[:, :, :, :, 1])
        nc.vector.tensor_copy(out=tok4[:], in_=tok2[:])
        nc.vector.tensor_add(out=tok4[:, :, :, 1], in0=tok4[:, :, :, 1], in1=eye5[:, :, :, 0, 1])
        nc.vector.tensor_add(out=tok4[:, 1:4, :, 0], in0=tok4[:, 1:4, :, 0], in1=eye5[:, 0:3, :, 1, 1])
        nc.vector.tensor_add(out=tok4[:, :, :, 0], in0=tok4[:, :, :, 0], in1=eye5[:, :, :, 1, 0])
        nc.vector.tensor_add(out=tok4[:, 0:3, :, 1], in0=tok4[:, 0:3, :, 1], in1=eye5[:, 1:4, :, 0, 0])
        rows4 = consts.tile([P, P], F32, name="rows4")
        rows2 = consts.tile([P, P], F32, name="rows2")
        for a in range(2):
            nc.vector.tensor_copy(out=rows4[:].rearrange("p (h b l a) -> p h b l a", h=4, b=8, l=2)[:, :, :, :, a], in_=tok4[:])
            nc.vector.tensor_copy(out=rows2[:].rearrange("p (h b l a) -> p h b l a", h=4, b=8, l=2)[:, :, :, :, a], in_=tok2[:])
        padded = consts.tile([P, 4, 18], F32, name="padded")
        nc.vector.memset(padded[:], 0.0)

        regroup_w(0, HEAD_SCALAR_COLS)
        for nth in range(1, HEAD_PASSES):
            regroup_w(nth, HEAD_SCALAR_COLS)
            quantise_w(nth - 1)

        gk = consts.tile([P, 80], F32, name="gk")
        bk = consts.tile([P, 80], F32, name="bk")
        for raw, dst, nm in ((graw, gk, "gf"), (braw, bk, "bf")):
            wide = consts.tile([P, P], F32, name=nm)
            nc.vector.tensor_copy(out=wide[:], in_=raw[:])
            pt = tp_pool.tile([P, 4, P], F32, name="tp")
            nc.tensor.transpose(out=pt[:, 0, :], in_=wide[:], identity=eye[:])
            nc.vector.tensor_copy(out=dst[:], in_=pt[:, 0, 0:80])
        quantise_w(HEAD_PASSES - 1)

        st6 = consts.tile([P, 16, 2, 6], F32, name="st6")
        for c_half in range(2):
            for cell_col in range(16):
                nc.vector.bn_stats(
                    out=st6[:, cell_col, c_half, :], in_=xc[:, 4 * c_half:4 * c_half + 4, :, 8 * cell_col:8 * cell_col + 8]
                )
        xc_flat = xc[:].rearrange("p c q w -> p (c q w)")
        for c in range(C):
            for rot, dst in ((rot_up, xu), (rot_dn, xd)):
                ps = tp_pool.tile([P, 1024], BF16, name="tp")
                for bank_half in range(2):
                    lo = 1024 * c + 512 * bank_half
                    nc.tensor.matmul(
                        out=ps[:, 512 * bank_half:512 * bank_half + 512], lhsT=rot[:], rhs=xc_flat[:, lo:lo + 512], start=True, stop=True
                    )
                nc.scalar.copy(out=dst[:].rearrange("p c q w -> p (c q w)")[:, 1024 * c:1024 * c + 1024], in_=ps[:])
        groups = st6[:].rearrange("p d f (e v) -> p d (f e) v", e=2)
        cells = consts.tile([P, 2, 16], F32, name="cells")
        sqm = consts.tile([P, 16, 4], F32, name="sqm")
        s2 = consts.tile([P, 16], F32, name="s2")
        m2 = consts.tile([P, 16], F32, name="m2")
        nc.vector.tensor_reduce(out=cells[:, 0, :], in_=groups[:, :, :, 1], axis=AX.X, op=ALU.add)
        nc.vector.tensor_mul(out=sqm[:], in0=groups[:, :, :, 1], in1=groups[:, :, :, 1])
        nc.vector.tensor_reduce(out=m2[:], in_=groups[:, :, :, 2], axis=AX.X, op=ALU.add)
        nc.vector.tensor_reduce(out=s2[:], in_=sqm[:], axis=AX.X, op=ALU.add)
        nc.vector.scalar_tensor_tensor(out=cells[:, 1, :], in0=s2[:], scalar=128.0, in1=m2[:], op0=ALU.mult, op1=ALU.add)
        st = tp_pool.tile([P, 4, P], F32, name="tp")
        nc.tensor.matmul(out=st[:, 0, 0:32], lhsT=rows4[:], rhs=cells[:].rearrange("p f d -> p (f d)"), start=True, stop=True)
        nc.tensor.matmul(out=st[:, 0, 32:64], lhsT=rows2[:], rhs=cells[:].rearrange("p f d -> p (f d)"), start=True, stop=True)
        nc.vector.tensor_copy(out=padded[:, :, 1:17], in_=st[:, 0, 0:64].rearrange("p (f d) -> p f d", d=16))
        pairs = consts.tile([P, 2, 9], F32, name="pairs")
        inner = consts.tile([P, 2, 8], F32, name="inner")
        tot = consts.tile([P, 2, 8], F32, name="tot")
        nc.vector.tensor_add(out=pairs[:], in0=padded[:, 0:2, 0:18:2], in1=padded[:, 0:2, 1:18:2])
        nc.vector.tensor_add(out=inner[:], in0=padded[:, 2:4, 1:17:2], in1=padded[:, 2:4, 2:18:2])
        nc.vector.tensor_add(out=tot[:], in0=pairs[:, :, 0:8], in1=pairs[:, :, 1:9])
        nc.vector.tensor_add(out=tot[:], in0=tot[:], in1=inner[:])
        small = {}
        for nm in ("mean", "msq", "var", "std", "r0", "nt", "rstd", "nmr"):
            small[nm] = consts.tile([P, 8], F32, name=nm)
        mean, msq, var, std, r0, nt, rstd, nmr = (small[nm] for nm in ("mean", "msq", "var", "std", "r0", "nt", "rstd", "nmr"))
        nc.vector.tensor_scalar_mul(out=mean[:], in0=tot[:, 0, :], scalar1=128.0 / PD)
        nc.vector.tensor_mul(out=msq[:], in0=mean[:], in1=mean[:])
        nc.vector.scalar_tensor_tensor(out=var[:], in0=tot[:, 1, :], scalar=1.0 / PD, in1=msq[:], op0=ALU.mult, op1=ALU.subtract)
        nc.vector.tensor_scalar(out=var[:], in0=var[:], scalar1=0.0, scalar2=EPS, op0=ALU.max, op1=ALU.add)
        nc.scalar.sqrt(out=std[:], in_=var[:])
        nc.vector.reciprocal(out=r0[:], in_=std[:])
        nc.vector.tensor_mul(out=nt[:], in0=r0[:], in1=r0[:])
        nc.vector.tensor_mul(out=nt[:], in0=nt[:], in1=var[:])
        nc.vector.tensor_scalar(out=nt[:], in0=nt[:], scalar1=-0.5, scalar2=1.5, op0=ALU.mult, op1=ALU.add)
        nc.vector.tensor_mul(out=rstd[:], in0=r0[:], in1=nt[:])
        nc.vector.scalar_tensor_tensor(out=nmr[:], in0=mean[:], scalar=-1.0, in1=rstd[:], op0=ALU.mult, op1=ALU.mult)

        def affine(on_scalar, dst, src, scale, bias):
            if on_scalar:
                nc.scalar.activation(out=dst, in_=src, func=ACT.Identity, bias=bias, scale=scale)
            else:
                nc.vector.tensor_scalar(out=dst, in0=src, scalar1=scale, scalar2=bias, op0=ALU.mult, op1=ALU.add)

        strips = {}

        def normalise(strip, n_scalar):
            j = 4 * (strip // 16) + strip % 4
            row_pair = (strip % 16) // 4
            xh = xh_pool.tile([P, 128 * RUNS_PER_STRIP], F32, name="xh")
            view = xh[:].rearrange("p (q e s c) -> p q e s c", q=2, e=16, s=5)
            for s, (di, dj) in enumerate(SHIFTS):
                source = (xu, xc, xd)[di + 1]
                col0 = 16 * j + 8 * dj
                lo = 8 if col0 < 0 else 0
                hi = 8 if col0 + 16 > HW else 16
                on_scalar = s >= 5 - n_scalar
                for c4 in range(2):
                    src = source[:, 4 * c4:4 * c4 + 4, 2 * row_pair:2 * row_pair + 2, col0 + lo:col0 + hi].rearrange("p c q e -> p q e c")
                    affine(on_scalar, view[:, :, lo:hi, s, 4 * c4:4 * c4 + 4], src, rstd[:, j:j + 1], nmr[:, j:j + 1])
                    if hi - lo < 16:
                        affine(on_scalar, view[:, :, 8 - lo:24 - hi, s, 4 * c4:4 * c4 + 4], src, 0.0, nmr[:, j:j + 1])
            strips[strip] = xh

        banks, planes, grouped, z_codes, acc = {}, {}, {}, {}, {}

        def transposes(u):
            banks[u] = []
            for t in range(4):
                nth_run = 4 * u + t
                pt = tp_pool.tile([P, 4, P], F32, name="tp")
                for jj in range(4):
                    nc.tensor.transpose(
                        out=pt[:, jj, :],
                        in_=strips[4 * (nth_run // RUNS_PER_STRIP) + jj][:, P * (nth_run % RUNS_PER_STRIP):P * (nth_run % RUNS_PER_STRIP) + P],
                        identity=perm[:],
                    )
                banks[u].append(pt)

        def evacuate(u):
            zp = zp_pool.tile([P, 2, 4, 256], BF16, name="zp")
            for t, pt in enumerate(banks.pop(u)):
                for a in range(2):
                    col = 40 * a + 4 * (u % 10) + t
                    affine(True, zp[:, a, t, :].rearrange("p (j m) -> p j m", j=4), pt[:, :, 64 * a:64 * a + 64],
                           gk[:, col:col + 1], bk[:, col:col + 1])
            planes[u] = zp

        def regroup_z(u):
            zi = zi_pool.tile([P, 2, 256, 4], BF16, name="zi", align_bytes=64)
            nc.vector.tensor_copy(
                out=zi[:].rearrange("p a (c i) t -> p a c t i", i=4), in_=planes.pop(u)[:].rearrange("p a t (c i) -> p a c t i", i=4)
            )
            grouped[u] = zi

        def quantise_z(u):
            zc = zc_pool.tile([P, 512], U32, name="zc", align_bytes=64)
            zs = zc_pool.tile([P, 512], U8, name="zs", align_bytes=64)
            nc.vector.quantize_mx(out=zc[:].bitcast(FP8X4), scales=zs[:], in_=grouped.pop(u)[:].rearrange("p a m t -> p (a m t)"))
            z_codes[u] = (zc, zs)

        def multiply(u):
            mu = u % 10
            if mu == 0:
                for bank in range(4):
                    acc[bank] = acc_pool.tile([P, 512], F32, name="acc%d" % bank)
            zc, zs = z_codes.pop(u)
            for tt in range(2):
                for a in range(2):
                    g = 10 * a + mu
                    cols = slice(256 * a + P * tt, 256 * a + P * tt + P)
                    for dst, lo, hi in ((acc[2 * tt], 0, 512), (acc[2 * tt + 1], 512, 768)):
                        nc.tensor.matmul_mx(
                            out=dst[:, 0:hi - lo],
                            lhsT=zc[:, cols].bitcast(FP8X4),
                            lhsT_scale=zs[:, cols],
                            rhs=w_codes[g][:, lo:hi].bitcast(FP8X4),
                            rhs_scale=w_scales[g][:, lo:hi],
                            start=(mu == 0 and a == 0),
                            stop=(mu == 9 and a == 1),
                        )

        out_rows = out.rearrange("b (i j) n -> j (b i) n", j=8)

        def finish(half):
            for tt in range(2):
                o = o_pool.tile([P, DIM], F32, name="o")
                nc.vector.tensor_tensor(out=o[:, 0:512], in0=acc[2 * tt][:], in1=b1b[:, 0:512], op=ALU.add)
                nc.vector.tensor_tensor(out=o[:, 512:768], in0=acc[2 * tt + 1][:, 0:256], in1=b1b[:, 512:768], op=ALU.add)
                for jl in range(2):
                    nc.sync.dma_start(out=out_rows[4 * half + 2 * tt + jl], in_=o[64 * jl:64 * jl + 64, :])

        for strip in range(LEAD_STRIPS):
            normalise(strip, 2)
        made = LEAD_STRIPS
        waiting = []

        def then_quantise(job):
            if waiting:
                waiting.pop()()
            if job is not None:
                waiting.append(job)

        for step in range(UNITS + 3):
            passes = range(min(HEAD_PASSES + (3 * step + 1) // 2, PASSES), min(HEAD_PASSES + (3 * step + 4) // 2, PASSES))
            if 2 <= step < UNITS + 2:
                regroup_z(step - 2)
                then_quantise(lambda u=step - 2: quantise_z(u))
            for nth in passes:
                regroup_w(nth, BODY_SCALAR_COLS)
                then_quantise(lambda nth=nth: quantise_w(nth))
            if step == 8:
                nc.sync.dma_start(out=b1b[:], in_=b1.partition_broadcast(P))
            if 1 <= step < UNITS + 1:
                evacuate(step - 1)
            if step >= 3:
                multiply(step - 3)
                if step - 3 in (9, 19):
                    finish((step - 3) // 10)
            if step < UNITS:
                transposes(step)
            target = min(STRIPS, LEAD_STRIPS + (8 * (step + 1) + 2) // 5)
            while made < target:
                normalise(made, 1 + 2 * len(passes))
                made += 1
            then_quantise(None)
